import numpy as np
import ml_dtypes


def mxq(x, axis, fmt="e4m3"):
    dtype, down = {"e4m3": (ml_dtypes.float8_e4m3fn, 7), "e5m2": (ml_dtypes.float8_e5m2, 14)}[fmt]
    v = np.moveaxis(np.asarray(x, np.float32).astype(ml_dtypes.bfloat16).astype(np.float64), axis, -1)
    blocks = v.reshape(v.shape[:-1] + (-1, 32))
    amax = np.abs(blocks).max(-1, keepdims=True)
    byte = np.maximum(np.where(amax > 0, np.frexp(amax)[1] - 1 + 127, 0) - down, 1)
    scale = np.exp2(byte - 127.0)
    codes = (blocks / scale).astype(np.float32).astype(dtype).astype(np.float64)
    return np.moveaxis((codes * scale).reshape(v.shape), -1, axis)


WIDE = False


def mx_kscale(k):
    if not WIDE:
        return np.ones(k)
    levels = np.array([20, -20, 10, -10, 0])
    a = np.random.permutation(np.resize(levels, k // 512 * 4)).reshape(k // 512, 4)
    idx = np.arange(k)
    return np.exp2(a[idx // 512, idx % 128 // 32])


BF16 = ml_dtypes.bfloat16


def bf(x):
    return np.asarray(x, np.float32).astype(BF16)


def f64(x):
    return np.asarray(x).astype(np.float64)


N, DI, DO, M = 128, 256, 512, 4
NB = 19


def mixt(cb, tq):
    rest = tq.shape[2:]
    y = cb @ np.moveaxis(tq, 1, 0).reshape(DO, -1)
    return np.moveaxis(y.reshape((DI, N) + rest), 0, 1)


def setup_inputs():
    u = mx_kscale(DO)
    gain = np.concatenate([np.ones(1), np.full(9, 1.0 / np.sqrt(M)), np.full(9, 1.0 / M)])
    x = np.random.standard_normal((N, DI, M, M, M))
    coefs = np.random.standard_normal((DI, DO, NB)) * (0.5 / np.sqrt(DI)) * gain / u[None, :, None]
    bias = np.random.standard_normal((1, DO, 1, 1, 1)) * 0.5
    g = np.random.standard_normal((N, DO, M, M, M)) * np.exp2(np.random.randint(-12, 1, (N, 1, M, M, M))) * 4.0 * u[None, :, None, None, None]
    return {"x": bf(x), "coefs": bf(coefs), "bias": bf(bias), "grad_out": bf(g)}


def reference(x, coefs, bias, grad_out):
    g = f64(grad_out)
    cq = mxq(f64(coefs), 1, "e4m3")
    out = mixt(cq[:, :, 0], mxq(g, 1, "e5m2"))
    for p in range(3):
        gq = mxq(g.sum(axis=2 + p), 1, "e5m2")
        for a in range(3):
            out = out + np.expand_dims(mixt(cq[:, :, 1 + 3 * a + p], gq), 2 + a)
    for p, axes in enumerate(((3, 4), (2, 4), (2, 3))):
        wq = mxq(g.sum(axis=axes), 1, "e5m2")
        for a in range(3):
            shape = [N, DI, 1, 1, 1]
            shape[4 - a] = M
            out = out + mixt(cq[:, :, 10 + 3 * a + p], wq).reshape(shape)
    return out

@@ -1,0 +1,232 @@
+from contextlib import ExitStack
+
+import concourse.mybir as mybir
+
+FLOPS = 2 * 256 * 512 * (8192 + 9 * 2048 + 9 * 512)
+BYTES = 256 * 512 * 19 * 2 + 128 * 512 * 64 * 2 + 128 * 256 * 64 * 4
+
+BF16 = mybir.dt.bfloat16
+F32 = mybir.dt.float32
+U32 = mybir.dt.uint32
+U8 = mybir.dt.uint8
+E4 = mybir.dt.float8_e4m3fn_x4
+E5 = mybir.dt.float8_e5m2_x4
+ADD = mybir.AluOpType.add
+AX = mybir.AxisListType
+
+P = 128
+NB = 19
+CH = 16
+NCH = 128 // CH
+DP = 32
+GBUFS = 3
+
+
+def tile_seteq3to3_t_kernel(tc, x, coefs, bias, grad_out, out):
+    nc = tc.nc
+    with ExitStack() as ctx:
+        keep = ctx.enter_context(tc.tile_pool(name="keep", bufs=1))
+        cw = ctx.enter_context(tc.tile_pool(name="cw", bufs=4))
+        psa = ctx.enter_context(tc.psum_pool(name="psa", bufs=4))
+        psb = ctx.enter_context(tc.psum_pool(name="psb", bufs=4))
+
+        gcodes = keep.tile([P, 4, 4, 512], U32, name="gcodes", align_bytes=64)
+        gscale = keep.tile([P, 4, 4, 512], U8, name="gscale", align_bytes=64)
+        Gcodes = [keep.tile([P, 2048], U32, name="Gcodes%d" % q, align_bytes=64) for q in range(3)]
+        Gscale = [keep.tile([P, 2048], U8, name="Gscale%d" % q, align_bytes=64) for q in range(3)]
+        Wcodes = [keep.tile([P, 512], U32, name="Wcodes%d" % q, align_bytes=64) for q in range(3)]
+        Wscale = [keep.tile([P, 512], U8, name="Wscale%d" % q, align_bytes=64) for q in range(3)]
+        ccodes = [keep.tile([P, NB * P], U32, name="ccodes%d" % c, align_bytes=64) for c in range(2)]
+        cscale = [keep.tile([P, NB * P], U8, name="cscale%d" % c, align_bytes=64) for c in range(2)]
+        cin = [None, None]
+        craws = {}
+
+        def coef_load(c, dp):
+            d0 = c * P + dp * DP
+            craw = cw.tile([P, DP, 76], BF16, tag="craw", name="craw%d_%d" % (c, dp))
+            nc.sync.dma_start(out=craw[:], in_=coefs[d0:d0 + DP].rearrange("d (p t) b -> p d (t b)", t=4))
+            craws[(c, dp)] = craw
+
+        def coef_piece(c, dp):
+            if dp == 0:
+                cin[c] = keep.tile([P, NB, P, 4], BF16, name="cin%d" % c, tag="cin", align_bytes=64)
+            nc.scalar.copy(
+                out=cin[c][:, :, dp * DP:(dp + 1) * DP, :],
+                in_=craws[(c, dp)][:].rearrange("p d (t b) -> p b d t", t=4))
+
+        def coef_quant(c):
+            flat = cin[c][:].rearrange("p b d t -> p (b d t)")
+            w0 = 0
+            for width in (4096, 4096, 1024, 512):
+                nc.vector.quantize_mx(
+                    out=ccodes[c][:, w0 // 4:(w0 + width) // 4].bitcast(E4),
+                    scales=cscale[c][:, w0 // 4:(w0 + width) // 4],
+                    in_=flat[:, w0:w0 + width])
+                w0 += width
+
+        with ExitStack() as ph1:
+            gpool = ph1.enter_context(tc.tile_pool(name="gpool", bufs=GBUFS))
+            work = ph1.enter_context(tc.tile_pool(name="work", bufs=2))
+            l2pool = ph1.enter_context(tc.tile_pool(name="l2pool", bufs=4))
+            gts = {}
+
+            def g_load(ch):
+                g_n = gpool.tile([P, CH, 256], BF16, tag="g", name="g%d" % ch)
+                nc.sync.dma_start(
+                    out=g_n[:],
+                    in_=grad_out[ch * CH:(ch + 1) * CH].rearrange("n (p t) i j k -> p n (t i j k)", t=4))
+                gts[ch] = g_n
+
+            for ch in range(4):
+                if ch < GBUFS:
+                    g_load(ch)
+                coef_load(0, ch)
+
+            for ch in range(NCH):
+                n0 = ch * CH
+                g_t = gts[ch]
+                g5 = g_t[:].rearrange("p n (t i c) -> p n t i c", t=4, i=4)
+
+                flat = g_t[:].rearrange("p n x -> p (n x)")
+                gf = []
+                for q, c1 in enumerate((32, 8, 2)):
+                    v1 = flat.rearrange("p (m h c) -> p m h c", h=2, c=c1)
+                    l1 = work.tile([P, 2048], F32, tag="l1")
+                    nc.vector.tensor_tensor(
+                        out=l1[:].rearrange("p (m c) -> p m c", c=c1), in0=v1[:, :, 0, :], in1=v1[:, :, 1, :], op=ADD)
+                    v2 = l1[:].rearrange("p (m h c) -> p m h c", h=2, c=c1 // 2)
+                    l2 = l2pool.tile([P, 1024], F32, tag="l2", name="l2_%d_%d" % (ch, q))
+                    nc.vector.tensor_tensor(
+                        out=l2[:].rearrange("p (m c) -> p m c", c=c1 // 2), in0=v2[:, :, 0, :], in1=v2[:, :, 1, :], op=ADD)
+                    gf.append(l2)
+                gq = work.tile([P, 3, CH, 64], BF16, tag="gq", align_bytes=64)
+                for q in range(3):
+                    nc.scalar.copy(
+                        out=gq[:, q].rearrange("p n (c t) -> p n c t", t=4),
+                        in_=gf[q][:].rearrange("p (n t c) -> p n c t", t=4, c=16))
+                wst = work.tile([P, 3, CH, 16], BF16, tag="wst", align_bytes=64)
+                gv0 = gf[0][:].rearrange("p (n t q r) -> p n t q r", t=4, q=4, r=4)
+                gv1 = gf[1][:].rearrange("p (n t q r) -> p n t q r", t=4, q=4, r=4)
+                with nc.allow_low_precision(reason="summed in float32 inside the engine, rounded once to bfloat16"):
+                    nc.vector.tensor_reduce(
+                        out=wst[:, 0].rearrange("p n (q t) -> p n q t", t=4),
+                        in_=gv1.rearrange("p n t q r -> p n q t r"), axis=AX.X, op=ADD)
+                    nc.vector.tensor_reduce(
+                        out=wst[:, 1].rearrange("p n (q t) -> p n q t", t=4),
+                        in_=gv0.rearrange("p n t q r -> p n q t r"), axis=AX.X, op=ADD)
+                    nc.vector.tensor_reduce(
+                        out=wst[:, 2].rearrange("p n (r t) -> p n r t", t=4),
+                        in_=gv0.rearrange("p n t q r -> p n r t q"), axis=AX.X, op=ADD)
+
+                gr = work.tile([P, 4, CH, 16, 4], BF16, tag="gr", align_bytes=64)
+                for i in range(4):
+                    nc.scalar.copy(out=gr[:, i], in_=g5[:, :, :, i, :].rearrange("p n t c -> p n c t"))
+
+                gsl = slice(n0 * 16, (n0 + CH) * 16)
+                for q in range(3):
+                    nc.vector.quantize_mx(
+                        out=Gcodes[q][:, gsl].bitcast(E5), scales=Gscale[q][:, gsl],
+                        in_=gq[:, q].rearrange("p n x -> p (n x)"))
+                wsl = slice(n0 * 4, (n0 + CH) * 4)
+                for q in range(3):
+                    nc.vector.quantize_mx(
+                        out=Wcodes[q][:, wsl].bitcast(E5), scales=Wscale[q][:, wsl],
+                        in_=wst[:, q].rearrange("p n x -> p (n x)"))
+                nb = n0 // 32
+                hsl = slice((n0 % 32) * 16, (n0 % 32 + CH) * 16)
+                for i in range(4):
+                    nc.vector.quantize_mx(
+                        out=gcodes[:, nb, i, hsl].bitcast(E5), scales=gscale[:, nb, i, hsl],
+                        in_=gr[:, i].rearrange("p n c t -> p (n c t)"))
+
+                if ch + GBUFS < NCH:
+                    g_load(ch + GBUFS)
+                if ch < 4:
+                    coef_piece(0, ch)
+                    coef_load(1, ch)
+                else:
+                    coef_piece(1, ch - 4)
+                if ch == 3:
+                    coef_quant(0)
+
+        def mx_group(ps, c, terms):
+            last = len(terms) - 1
+            for idx, (b, rc, rs) in enumerate(terms):
+                nc.tensor.matmul_mx(
+                    out=ps,
+                    lhsT=ccodes[c][:, b * P:(b + 1) * P].bitcast(E4),
+                    lhsT_scale=cscale[c][:, b * P:(b + 1) * P],
+                    rhs=rc.bitcast(E5), rhs_scale=rs,
+                    start=(idx == 0), stop=(idx == last))
+
+        with ExitStack() as ph2:
+            work2 = ph2.enter_context(tc.tile_pool(name="work2", bufs=2))
+            xpool = ph2.enter_context(tc.tile_pool(name="xpool", bufs=3))
+
+            def gterms(nb):
+                cs = slice(nb * 512, nb * 512 + 512)
+                return [(Gcodes[q][:, cs], Gscale[q][:, cs]) for q in range(3)]
+
+            def u_terms(c):
+                usb = []
+                for a in range(3):
+                    pu = psb.tile([P, 512], F32, tag="b")
+                    mx_group(pu[:], c, [(10 + 3 * a + q, Wcodes[q][:], Wscale[q][:]) for q in range(3)])
+                    ut = work2.tile([P, P, 4], F32, name="u%d_%d" % (a, c), tag="u%d" % a)
+                    nc.scalar.copy(out=ut[:].rearrange("p n q -> p (n q)"), in_=pu[:])
+                    usb.append(ut)
+                u02 = work2.tile([P, P, 4, 4], F32, name="u02_%d" % c, tag="u02")
+                nc.gpsimd.tensor_tensor(
+                    out=u02[:], in0=usb[0][:].unsqueeze(2).to_broadcast([P, P, 4, 4]),
+                    in1=usb[2][:].unsqueeze(3).to_broadcast([P, P, 4, 4]), op=ADD)
+                return u02, usb[1]
+
+            def h_terms(c, nb, u02, u1):
+                ns = slice(nb * 32, nb * 32 + 32)
+                gt = gterms(nb)
+                p1 = psb.tile([P, 512], F32, tag="b")
+                mx_group(p1[:], c, [(4 + q, gt[q][0], gt[q][1]) for q in range(3)])
+                h1 = work2.tile([P, 32, 4, 4], F32, tag="h1")
+                nc.vector.tensor_tensor(
+                    out=h1[:], in0=p1[:].rearrange("p (n i k) -> p n i k", i=4, k=4), in1=u02[:, ns], op=ADD)
+                p2 = psb.tile([P, 512], F32, tag="b")
+                mx_group(p2[:], c, [(7 + q, gt[q][0], gt[q][1]) for q in range(3)])
+                h2 = work2.tile([P, 32, 4, 4], F32, tag="h2")
+                nc.vector.tensor_tensor(
+                    out=h2[:], in0=p2[:].rearrange("p (n i j) -> p n i j", i=4, j=4),
+                    in1=u1[:, ns, :].unsqueeze(2).to_broadcast([P, 32, 4, 4]), op=ADD)
+                xt = xpool.tile([P, 32, 4, 4, 4], F32, tag="xt", name="xt%d_%d" % (c, nb))
+                nc.gpsimd.tensor_tensor(
+                    out=xt[:].rearrange("p n i j k -> p (n i) j k"),
+                    in0=h1[:].rearrange("p n i k -> p (n i) k").unsqueeze(2).to_broadcast([P, P, 4, 4]),
+                    in1=h2[:].rearrange("p n i j -> p (n i) j").unsqueeze(3).to_broadcast([P, P, 4, 4]),
+                    op=ADD)
+                return xt
+
+            def main_terms(c, nb, xt):
+                ns = slice(nb * 32, nb * 32 + 32)
+                gt = gterms(nb)
+                for i in range(4):
+                    pm = psa.tile([P, 512], F32, tag="a")
+                    mx_group(pm[:], c, [(0, gcodes[:, nb, i, :], gscale[:, nb, i, :])]
+                             + [(1 + q, gt[q][0], gt[q][1]) for q in range(3)])
+                    xi = xt[:, :, i, :, :].rearrange("p n j k -> p n (j k)")
+                    nc.vector.tensor_tensor(
+                        out=xi, in0=pm[:].rearrange("p (n x) -> p n x", x=16), in1=xi, op=ADD)
+                nc.sync.dma_start(
+                    out=out[ns, c * P:(c + 1) * P].rearrange("n d i j k -> d n (i j k)"),
+                    in_=xt[:].rearrange("p n i j k -> p n (i j k)"))
+
+            steps = [(c, nb) for c in range(2) for nb in range(4)]
+            us = {0: u_terms(0)}
+            xts = {0: h_terms(0, 0, us[0][0], us[0][1])}
+            for s in range(8):
+                c, nb = steps[s]
+                if s == 0:
+                    coef_quant(1)
+                if s == 3:
+                    us[1] = u_terms(1)
+                if s + 1 < 8:
+                    c2, nb2 = steps[s + 1]
+                    xts[s + 1] = h_terms(c2, nb2, us[c2][0], us[c2][1])
+                main_terms(c, nb, xts[s])

@@ -1,12 +1,14 @@
 from contextlib import ExitStack
 
 import concourse.mybir as mybir
+from concourse.masks import make_identity
 
 FLOPS = 2 * 256 * 512 * (8192 + 9 * 2048 + 9 * 512)
 BYTES = 256 * 512 * 19 * 2 + 128 * 512 * 64 * 2 + 128 * 256 * 64 * 4
 
 BF16 = mybir.dt.bfloat16
 F32 = mybir.dt.float32
+I32 = mybir.dt.int32
 U32 = mybir.dt.uint32
 U8 = mybir.dt.uint8
 E4 = mybir.dt.float8_e4m3fn_x4
@@ -18,7 +20,6 @@ P = 128
 NB = 19
 CH = 16
 NCH = 128 // CH
-DP = 32
 GBUFS = 3
 
 
@@ -26,128 +27,122 @@ def tile_seteq3to3_t_kernel(tc, x, coefs, bias, grad_out, out):
     nc = tc.nc
     with ExitStack() as ctx:
         keep = ctx.enter_context(tc.tile_pool(name="keep", bufs=1))
-        cw = ctx.enter_context(tc.tile_pool(name="cw", bufs=4))
-        psa = ctx.enter_context(tc.psum_pool(name="psa", bufs=4))
-        psb = ctx.enter_context(tc.psum_pool(name="psb", bufs=4))
+        work = ctx.enter_context(tc.tile_pool(name="work", bufs=2))
+        gpool = ctx.enter_context(tc.tile_pool(name="gpool", bufs=GBUFS))
+        l2pool = ctx.enter_context(tc.tile_pool(name="l2pool", bufs=4))
+        xpool = ctx.enter_context(tc.tile_pool(name="xpool", bufs=3))
+        psa = ctx.enter_context(tc.psum_pool(name="psa", bufs=3))
+        psb = ctx.enter_context(tc.psum_pool(name="psb", bufs=3))
+        psc = ctx.enter_context(tc.psum_pool(name="psc", bufs=2))
 
-        gcodes = keep.tile([P, 4, 4, 512], U32, name="gcodes", align_bytes=64)
-        gscale = keep.tile([P, 4, 4, 512], U8, name="gscale", align_bytes=64)
-        Gcodes = [keep.tile([P, 2048], U32, name="Gcodes%d" % q, align_bytes=64) for q in range(3)]
-        Gscale = [keep.tile([P, 2048], U8, name="Gscale%d" % q, align_bytes=64) for q in range(3)]
+        ident = keep.tile([P, P], BF16, name="ident")
+        make_identity(nc, ident[:])
+
         Wcodes = [keep.tile([P, 512], U32, name="Wcodes%d" % q, align_bytes=64) for q in range(3)]
         Wscale = [keep.tile([P, 512], U8, name="Wscale%d" % q, align_bytes=64) for q in range(3)]
+        for q in range(3):
+            nc.vector.memset(Wcodes[q][:].bitcast(I32), 0)
+            nc.vector.memset(Wscale[q][:].bitcast(I32), 0)
         ccodes = [keep.tile([P, NB * P], U32, name="ccodes%d" % c, align_bytes=64) for c in range(2)]
         cscale = [keep.tile([P, NB * P], U8, name="cscale%d" % c, align_bytes=64) for c in range(2)]
-        cin = [None, None]
+
+        gts = {}
         craws = {}
 
-        def coef_load(c, dp):
-            d0 = c * P + dp * DP
-            craw = cw.tile([P, DP, 76], BF16, tag="craw", name="craw%d_%d" % (c, dp))
-            nc.sync.dma_start(out=craw[:], in_=coefs[d0:d0 + DP].rearrange("d (p t) b -> p d (t b)", t=4))
-            craws[(c, dp)] = craw
+        def g_load(ch):
+            g_n = gpool.tile([P, CH, 256], BF16, tag="g", name="g%d" % ch)
+            nc.sync.dma_start(
+                out=g_n[:],
+                in_=grad_out[ch * CH:(ch + 1) * CH].rearrange("n (p t) i j k -> p n (t i j k)", t=4))
+            gts[ch] = g_n
 
-        def coef_piece(c, dp):
-            if dp == 0:
-                cin[c] = keep.tile([P, NB, P, 4], BF16, name="cin%d" % c, tag="cin", align_bytes=64)
-            nc.scalar.copy(
-                out=cin[c][:, :, dp * DP:(dp + 1) * DP, :],
-                in_=craws[(c, dp)][:].rearrange("p d (t b) -> p b d t", t=4))
+        def coef_load(c):
+            craw = keep.tile([P, 512 * NB], BF16, tag="craw", name="craw%d" % c)
+            nc.sync.dma_start(out=craw[:], in_=coefs[c * P:(c + 1) * P].rearrange("d s b -> d (s b)"))
+            craws[c] = craw
 
-        def coef_quant(c):
-            flat = cin[c][:].rearrange("p b d t -> p (b d t)")
-            w0 = 0
-            for width in (4096, 4096, 1024, 512):
+        def coef_stage(c):
+            cv = craws[c][:].rearrange("d (p y) -> d p y", y=4 * NB)
+            b0 = 0
+            for nbg in (8, 8, 2, 1):
+                cin = work.tile([P, nbg, P, 4], BF16, tag="cin", name="cin%d_%d" % (c, b0), align_bytes=64)
+                for b1 in range(0, nbg, 2):
+                    nb2 = min(2, nbg - b1)
+                    pc = psc.tile([P, nb2, 4, P], BF16, tag="c", name="pc%d_%d" % (c, b0 + b1))
+                    for bi in range(nb2):
+                        for t in range(4):
+                            nc.tensor.transpose(pc[:, bi, t, :], cv[:, :, t * NB + b0 + b1 + bi], ident[:])
+                    nc.scalar.copy(out=cin[:, b1:b1 + nb2], in_=pc[:].rearrange("p b t d -> p b d t"))
                 nc.vector.quantize_mx(
-                    out=ccodes[c][:, w0 // 4:(w0 + width) // 4].bitcast(E4),
-                    scales=cscale[c][:, w0 // 4:(w0 + width) // 4],
-                    in_=flat[:, w0:w0 + width])
-                w0 += width
+                    out=ccodes[c][:, b0 * P:(b0 + nbg) * P].bitcast(E4),
+                    scales=cscale[c][:, b0 * P:(b0 + nbg) * P],
+                    in_=cin[:].rearrange("p b d t -> p (b d t)"))
+                b0 += nbg
 
-        with ExitStack() as ph1:
-            gpool = ph1.enter_context(tc.tile_pool(name="gpool", bufs=GBUFS))
-            work = ph1.enter_context(tc.tile_pool(name="work", bufs=2))
-            l2pool = ph1.enter_context(tc.tile_pool(name="l2pool", bufs=4))
-            gts = {}
+        codes = {}
 
-            def g_load(ch):
-                g_n = gpool.tile([P, CH, 256], BF16, tag="g", name="g%d" % ch)
-                nc.sync.dma_start(
-                    out=g_n[:],
-                    in_=grad_out[ch * CH:(ch + 1) * CH].rearrange("n (p t) i j k -> p n (t i j k)", t=4))
-                gts[ch] = g_n
+        def chunk(ch):
+            n0 = ch * CH
+            nb = n0 // 32
+            if n0 % 32 == 0:
+                codes[nb] = (
+                    work.tile([P, 4, 512], U32, tag="gcodes", name="gcodes%d" % nb, align_bytes=64),
+                    work.tile([P, 4, 512], U8, tag="gscale", name="gscale%d" % nb, align_bytes=64),
+                    work.tile([P, 3, 512], U32, tag="Gcodes", name="Gcodes%d" % nb, align_bytes=64),
+                    work.tile([P, 3, 512], U8, tag="Gscale", name="Gscale%d" % nb, align_bytes=64))
+            gcodes, gscale, Gcodes, Gscale = codes[nb]
+            g_t = gts[ch]
+            g5 = g_t[:].rearrange("p n (t i c) -> p n t i c", t=4, i=4)
 
-            for ch in range(4):
-                if ch < GBUFS:
-                    g_load(ch)
-                coef_load(0, ch)
+            flat = g_t[:].rearrange("p n y -> p (n y)")
+            gf = []
+            for q, c1 in enumerate((32, 8, 2)):
+                v1 = flat.rearrange("p (m h c) -> p m h c", h=2, c=c1)
+                l1 = work.tile([P, 2048], F32, tag="l1")
+                nc.vector.tensor_tensor(
+                    out=l1[:].rearrange("p (m c) -> p m c", c=c1), in0=v1[:, :, 0, :], in1=v1[:, :, 1, :], op=ADD)
+                v2 = l1[:].rearrange("p (m h c) -> p m h c", h=2, c=c1 // 2)
+                l2 = l2pool.tile([P, 1024], F32, tag="l2", name="l2_%d_%d" % (ch, q))
+                nc.vector.tensor_tensor(
+                    out=l2[:].rearrange("p (m c) -> p m c", c=c1 // 2), in0=v2[:, :, 0, :], in1=v2[:, :, 1, :], op=ADD)
+                gf.append(l2)
+            gq = work.tile([P, 3, CH, 64], BF16, tag="gq", align_bytes=64)
+            for q in range(3):
+                nc.scalar.copy(
+                    out=gq[:, q].rearrange("p n (c t) -> p n c t", t=4),
+                    in_=gf[q][:].rearrange("p (n t c) -> p n c t", t=4, c=16))
+            wst = work.tile([P, 3, CH, 16], BF16, tag="wst", align_bytes=64)
+            gv0 = gf[0][:].rearrange("p (n t q r) -> p n t q r", t=4, q=4, r=4)
+            gv1 = gf[1][:].rearrange("p (n t q r) -> p n t q r", t=4, q=4, r=4)
+            with nc.allow_low_precision(reason="summed in float32 inside the engine, rounded once to bfloat16"):
+                nc.vector.tensor_reduce(
+                    out=wst[:, 0].rearrange("p n (q t) -> p n q t", t=4),
+                    in_=gv1.rearrange("p n t q r -> p n q t r"), axis=AX.X, op=ADD)
+                nc.vector.tensor_reduce(
+                    out=wst[:, 1].rearrange("p n (q t) -> p n q t", t=4),
+                    in_=gv0.rearrange("p n t q r -> p n q t r"), axis=AX.X, op=ADD)
+                nc.vector.tensor_reduce(
+                    out=wst[:, 2].rearrange("p n (r t) -> p n r t", t=4),
+                    in_=gv0.rearrange("p n t q r -> p n r t q"), axis=AX.X, op=ADD)
 
-            for ch in range(NCH):
-                n0 = ch * CH
-                g_t = gts[ch]
-                g5 = g_t[:].rearrange("p n (t i c) -> p n t i c", t=4, i=4)
+            gr = work.tile([P, 4, CH, 16, 4], BF16, tag="gr", align_bytes=64)
+            for i in range(4):
+                nc.scalar.copy(out=gr[:, i], in_=g5[:, :, :, i, :].rearrange("p n t c -> p n c t"))
 
-                flat = g_t[:].rearrange("p n x -> p (n x)")
-                gf = []
-                for q, c1 in enumerate((32, 8, 2)):
-                    v1 = flat.rearrange("p (m h c) -> p m h c", h=2, c=c1)
-                    l1 = work.tile([P, 2048], F32, tag="l1")
-                    nc.vector.tensor_tensor(
-                        out=l1[:].rearrange("p (m c) -> p m c", c=c1), in0=v1[:, :, 0, :], in1=v1[:, :, 1, :], op=ADD)
-                    v2 = l1[:].rearrange("p (m h c) -> p m h c", h=2, c=c1 // 2)
-                    l2 = l2pool.tile([P, 1024], F32, tag="l2", name="l2_%d_%d" % (ch, q))
-                    nc.vector.tensor_tensor(
-                        out=l2[:].rearrange("p (m c) -> p m c", c=c1 // 2), in0=v2[:, :, 0, :], in1=v2[:, :, 1, :], op=ADD)
-                    gf.append(l2)
-                gq = work.tile([P, 3, CH, 64], BF16, tag="gq", align_bytes=64)
-                for q in range(3):
-                    nc.scalar.copy(
-                        out=gq[:, q].rearrange("p n (c t) -> p n c t", t=4),
-                        in_=gf[q][:].rearrange("p (n t c) -> p n c t", t=4, c=16))
-                wst = work.tile([P, 3, CH, 16], BF16, tag="wst", align_bytes=64)
-                gv0 = gf[0][:].rearrange("p (n t q r) -> p n t q r", t=4, q=4, r=4)
-                gv1 = gf[1][:].rearrange("p (n t q r) -> p n t q r", t=4, q=4, r=4)
-                with nc.allow_low_precision(reason="summed in float32 inside the engine, rounded once to bfloat16"):
-                    nc.vector.tensor_reduce(
-                        out=wst[:, 0].rearrange("p n (q t) -> p n q t", t=4),
-                        in_=gv1.rearrange("p n t q r -> p n q t r"), axis=AX.X, op=ADD)
-                    nc.vector.tensor_reduce(
-                        out=wst[:, 1].rearrange("p n (q t) -> p n q t", t=4),
-                        in_=gv0.rearrange("p n t q r -> p n q t r"), axis=AX.X, op=ADD)
-                    nc.vector.tensor_reduce(
-                        out=wst[:, 2].rearrange("p n (r t) -> p n r t", t=4),
-                        in_=gv0.rearrange("p n t q r -> p n r t q"), axis=AX.X, op=ADD)
-
-                gr = work.tile([P, 4, CH, 16, 4], BF16, tag="gr", align_bytes=64)
-                for i in range(4):
-                    nc.scalar.copy(out=gr[:, i], in_=g5[:, :, :, i, :].rearrange("p n t c -> p n c t"))
-
-                gsl = slice(n0 * 16, (n0 + CH) * 16)
-                for q in range(3):
-                    nc.vector.quantize_mx(
-                        out=Gcodes[q][:, gsl].bitcast(E5), scales=Gscale[q][:, gsl],
-                        in_=gq[:, q].rearrange("p n x -> p (n x)"))
-                wsl = slice(n0 * 4, (n0 + CH) * 4)
-                for q in range(3):
-                    nc.vector.quantize_mx(
-                        out=Wcodes[q][:, wsl].bitcast(E5), scales=Wscale[q][:, wsl],
-                        in_=wst[:, q].rearrange("p n x -> p (n x)"))
-                nb = n0 // 32
-                hsl = slice((n0 % 32) * 16, (n0 % 32 + CH) * 16)
-                for i in range(4):
-                    nc.vector.quantize_mx(
-                        out=gcodes[:, nb, i, hsl].bitcast(E5), scales=gscale[:, nb, i, hsl],
-                        in_=gr[:, i].rearrange("p n c t -> p (n c t)"))
-
-                if ch + GBUFS < NCH:
-                    g_load(ch + GBUFS)
-                if ch < 4:
-                    coef_piece(0, ch)
-                    coef_load(1, ch)
-                else:
-                    coef_piece(1, ch - 4)
-                if ch == 3:
-                    coef_quant(0)
+            hsl = slice((n0 % 32) * 16, (n0 % 32 + CH) * 16)
+            for q in range(3):
+                nc.vector.quantize_mx(
+                    out=Gcodes[:, q, hsl].bitcast(E5), scales=Gscale[:, q, hsl],
+                    in_=gq[:, q].rearrange("p n y -> p (n y)"))
+            wsl = slice(n0 * 4, (n0 + CH) * 4)
+            for q in range(3):
+                nc.vector.quantize_mx(
+                    out=Wcodes[q][:, wsl].bitcast(E5), scales=Wscale[q][:, wsl],
+                    in_=wst[:, q].rearrange("p n y -> p (n y)"))
+            for i in range(4):
+                nc.vector.quantize_mx(
+                    out=gcodes[:, i, hsl].bitcast(E5), scales=gscale[:, i, hsl],
+                    in_=gr[:, i].rearrange("p n c t -> p (n c t)"))
 
         def mx_group(ps, c, terms):
             last = len(terms) - 1
@@ -159,74 +154,65 @@ def tile_seteq3to3_t_kernel(tc, x, coefs, bias, grad_out, out):
                     rhs=rc.bitcast(E5), rhs_scale=rs,
                     start=(idx == 0), stop=(idx == last))
 
-        with ExitStack() as ph2:
-            work2 = ph2.enter_context(tc.tile_pool(name="work2", bufs=2))
-            xpool = ph2.enter_context(tc.tile_pool(name="xpool", bufs=3))
+        def small_terms(c, nb):
+            gcodes, gscale, Gcodes, Gscale = codes[nb]
+            usb = []
+            for a in range(3):
+                pu = psb.tile([P, 512], F32, tag="b")
+                mx_group(pu[:], c, [(10 + 3 * a + q, Wcodes[q][:], Wscale[q][:]) for q in range(3)])
+                ut = work.tile([P, 32, 4], F32, name="u%d_%d_%d" % (a, c, nb), tag="u%d" % a)
+                nc.scalar.copy(out=ut[:].rearrange("p n q -> p (n q)"), in_=pu[:, nb * P:(nb + 1) * P])
+                usb.append(ut)
+            u02 = work.tile([P, 32, 4, 4], F32, tag="u02")
+            nc.gpsimd.tensor_tensor(
+                out=u02[:], in0=usb[0][:].unsqueeze(2).to_broadcast([P, 32, 4, 4]),
+                in1=usb[2][:].unsqueeze(3).to_broadcast([P, 32, 4, 4]), op=ADD)
+            p1 = psb.tile([P, 512], F32, tag="b")
+            mx_group(p1[:], c, [(4 + q, Gcodes[:, q, :], Gscale[:, q, :]) for q in range(3)])
+            h1 = work.tile([P, 32, 4, 4], F32, tag="h1")
+            nc.vector.tensor_tensor(
+                out=h1[:], in0=p1[:].rearrange("p (n i k) -> p n i k", i=4, k=4), in1=u02[:], op=ADD)
+            p2 = psb.tile([P, 512], F32, tag="b")
+            mx_group(p2[:], c, [(7 + q, Gcodes[:, q, :], Gscale[:, q, :]) for q in range(3)])
+            h2 = work.tile([P, 32, 4, 4], F32, tag="h2")
+            nc.vector.tensor_tensor(
+                out=h2[:], in0=p2[:].rearrange("p (n i j) -> p n i j", i=4, j=4),
+                in1=usb[1][:].unsqueeze(2).to_broadcast([P, 32, 4, 4]), op=ADD)
+            xt = xpool.tile([P, 32, 4, 4, 4], F32, tag="xt", name="xt%d_%d" % (c, nb))
+            nc.gpsimd.tensor_tensor(
+                out=xt[:].rearrange("p n i j k -> p (n i) j k"),
+                in0=h1[:].rearrange("p n i k -> p (n i) k").unsqueeze(2).to_broadcast([P, P, 4, 4]),
+                in1=h2[:].rearrange("p n i j -> p (n i) j").unsqueeze(3).to_broadcast([P, P, 4, 4]),
+                op=ADD)
+            return xt
 
-            def gterms(nb):
-                cs = slice(nb * 512, nb * 512 + 512)
-                return [(Gcodes[q][:, cs], Gscale[q][:, cs]) for q in range(3)]
-
-            def u_terms(c):
-                usb = []
-                for a in range(3):
-                    pu = psb.tile([P, 512], F32, tag="b")
-                    mx_group(pu[:], c, [(10 + 3 * a + q, Wcodes[q][:], Wscale[q][:]) for q in range(3)])
-                    ut = work2.tile([P, P, 4], F32, name="u%d_%d" % (a, c), tag="u%d" % a)
-                    nc.scalar.copy(out=ut[:].rearrange("p n q -> p (n q)"), in_=pu[:])
-                    usb.append(ut)
-                u02 = work2.tile([P, P, 4, 4], F32, name="u02_%d" % c, tag="u02")
-                nc.gpsimd.tensor_tensor(
-                    out=u02[:], in0=usb[0][:].unsqueeze(2).to_broadcast([P, P, 4, 4]),
-                    in1=usb[2][:].unsqueeze(3).to_broadcast([P, P, 4, 4]), op=ADD)
-                return u02, usb[1]
-
-            def h_terms(c, nb, u02, u1):
-                ns = slice(nb * 32, nb * 32 + 32)
-                gt = gterms(nb)
-                p1 = psb.tile([P, 512], F32, tag="b")
-                mx_group(p1[:], c, [(4 + q, gt[q][0], gt[q][1]) for q in range(3)])
-                h1 = work2.tile([P, 32, 4, 4], F32, tag="h1")
+        def main_terms(c, nb, xt):
+            gcodes, gscale, Gcodes, Gscale = codes[nb]
+            ns = slice(nb * 32, nb * 32 + 32)
+            for i in range(4):
+                pm = psa.tile([P, 512], F32, tag="a")
+                mx_group(pm[:], c, [(0, gcodes[:, i, :], gscale[:, i, :])]
+                         + [(1 + q, Gcodes[:, q, :], Gscale[:, q, :]) for q in range(3)])
+                xi = xt[:, :, i, :, :].rearrange("p n j k -> p n (j k)")
                 nc.vector.tensor_tensor(
-                    out=h1[:], in0=p1[:].rearrange("p (n i k) -> p n i k", i=4, k=4), in1=u02[:, ns], op=ADD)
-                p2 = psb.tile([P, 512], F32, tag="b")
-                mx_group(p2[:], c, [(7 + q, gt[q][0], gt[q][1]) for q in range(3)])
-                h2 = work2.tile([P, 32, 4, 4], F32, tag="h2")
-                nc.vector.tensor_tensor(
-                    out=h2[:], in0=p2[:].rearrange("p (n i j) -> p n i j", i=4, j=4),
-                    in1=u1[:, ns, :].unsqueeze(2).to_broadcast([P, 32, 4, 4]), op=ADD)
-                xt = xpool.tile([P, 32, 4, 4, 4], F32, tag="xt", name="xt%d_%d" % (c, nb))
-                nc.gpsimd.tensor_tensor(
-                    out=xt[:].rearrange("p n i j k -> p (n i) j k"),
-                    in0=h1[:].rearrange("p n i k -> p (n i) k").unsqueeze(2).to_broadcast([P, P, 4, 4]),
-                    in1=h2[:].rearrange("p n i j -> p (n i) j").unsqueeze(3).to_broadcast([P, P, 4, 4]),
-                    op=ADD)
-                return xt
+                    out=xi, in0=pm[:].rearrange("p (n y) -> p n y", y=16), in1=xi, op=ADD)
+            nc.sync.dma_start(
+                out=out[ns, c * P:(c + 1) * P].rearrange("n d i j k -> d n (i j k)"),
+                in_=xt[:].rearrange("p n i j k -> p n (i j k)"))
 
-            def main_terms(c, nb, xt):
-                ns = slice(nb * 32, nb * 32 + 32)
-                gt = gterms(nb)
-                for i in range(4):
-                    pm = psa.tile([P, 512], F32, tag="a")
-                    mx_group(pm[:], c, [(0, gcodes[:, nb, i, :], gscale[:, nb, i, :])]
-                             + [(1 + q, gt[q][0], gt[q][1]) for q in range(3)])
-                    xi = xt[:, :, i, :, :].rearrange("p n j k -> p n (j k)")
-                    nc.vector.tensor_tensor(
-                        out=xi, in0=pm[:].rearrange("p (n x) -> p n x", x=16), in1=xi, op=ADD)
-                nc.sync.dma_start(
-                    out=out[ns, c * P:(c + 1) * P].rearrange("n d i j k -> d n (i j k)"),
-                    in_=xt[:].rearrange("p n i j k -> p n (i j k)"))
-
-            steps = [(c, nb) for c in range(2) for nb in range(4)]
-            us = {0: u_terms(0)}
-            xts = {0: h_terms(0, 0, us[0][0], us[0][1])}
-            for s in range(8):
-                c, nb = steps[s]
-                if s == 0:
-                    coef_quant(1)
-                if s == 3:
-                    us[1] = u_terms(1)
-                if s + 1 < 8:
-                    c2, nb2 = steps[s + 1]
-                    xts[s + 1] = h_terms(c2, nb2, us[c2][0], us[c2][1])
-                main_terms(c, nb, xts[s])
+        g_load(0)
+        coef_load(0)
+        g_load(1)
+        g_load(2)
+        coef_stage(0)
+        coef_load(1)
+        coef_stage(1)
+        for ch in range(NCH):
+            chunk(ch)
+            if ch + GBUFS < NCH:
+                g_load(ch + GBUFS)
+            if ch % 2 == 1:
+                nb = ch // 2
+                xts = [small_terms(c, nb) for c in range(2)]
+                for c in range(2):
+                    main_terms(c, nb, xts[c])

@@ -27,157 +27,189 @@ def tile_seteq3to3_t_kernel(tc, x, coefs, bias, grad_out, out):
     nc = tc.nc
     with ExitStack() as ctx:
         keep = ctx.enter_context(tc.tile_pool(name="keep", bufs=1))
-        work = ctx.enter_context(tc.tile_pool(name="work", bufs=2))
-        gpool = ctx.enter_context(tc.tile_pool(name="gpool", bufs=GBUFS))
-        l2pool = ctx.enter_context(tc.tile_pool(name="l2pool", bufs=4))
-        xpool = ctx.enter_context(tc.tile_pool(name="xpool", bufs=3))
         psa = ctx.enter_context(tc.psum_pool(name="psa", bufs=3))
         psb = ctx.enter_context(tc.psum_pool(name="psb", bufs=3))
         psc = ctx.enter_context(tc.psum_pool(name="psc", bufs=2))
+        with ExitStack() as ph1:
+            work = ph1.enter_context(tc.tile_pool(name="work", bufs=2))
+            gpool = ph1.enter_context(tc.tile_pool(name="gpool", bufs=GBUFS))
+            l1pool = ph1.enter_context(tc.tile_pool(name="l1pool", bufs=3))
+            l2pool = ph1.enter_context(tc.tile_pool(name="l2pool", bufs=4))
 
-        ident = keep.tile([P, P], BF16, name="ident")
-        make_identity(nc, ident[:])
+            ident = keep.tile([P, P], BF16, name="ident")
+            make_identity(nc, ident[:])
 
-        Wcodes = [keep.tile([P, 512], U32, name="Wcodes%d" % q, align_bytes=64) for q in range(3)]
-        Wscale = [keep.tile([P, 512], U8, name="Wscale%d" % q, align_bytes=64) for q in range(3)]
-        for q in range(3):
-            nc.vector.memset(Wcodes[q][:].bitcast(I32), 0)
-            nc.vector.memset(Wscale[q][:].bitcast(I32), 0)
-        ccodes = [keep.tile([P, NB * P], U32, name="ccodes%d" % c, align_bytes=64) for c in range(2)]
-        cscale = [keep.tile([P, NB * P], U8, name="cscale%d" % c, align_bytes=64) for c in range(2)]
+            Wcodes = [keep.tile([P, 512], U32, name="Wcodes%d" % q, align_bytes=64) for q in range(3)]
+            Wscale = [keep.tile([P, 512], U8, name="Wscale%d" % q, align_bytes=64) for q in range(3)]
+            gcodes = keep.tile([P, 4, 4, 512], U32, name="gcodes", align_bytes=64)
+            gscale = keep.tile([P, 4, 4, 512], U8, name="gscale", align_bytes=64)
+            Gcodes = keep.tile([P, 3, 2048], U32, name="Gcodes", align_bytes=64)
+            Gscale = keep.tile([P, 3, 2048], U8, name="Gscale", align_bytes=64)
+            ccodes = [keep.tile([P, NB * P], U32, name="ccodes%d" % c, align_bytes=64) for c in range(2)]
+            cscale = [keep.tile([P, NB * P], U8, name="cscale%d" % c, align_bytes=64) for c in range(2)]
 
-        gts = {}
-        craws = {}
+            gts = {}
+            craws = {}
 
-        def g_load(ch):
-            g_n = gpool.tile([P, CH, 256], BF16, tag="g", name="g%d" % ch)
-            nc.sync.dma_start(
-                out=g_n[:],
-                in_=grad_out[ch * CH:(ch + 1) * CH].rearrange("n (p t) i j k -> p n (t i j k)", t=4))
-            gts[ch] = g_n
+            def g_load(ch):
+                g_n = gpool.tile([P, CH, 256], BF16, tag="g", name="g%d" % ch)
+                nc.sync.dma_start(
+                    out=g_n[:],
+                    in_=grad_out[ch * CH:(ch + 1) * CH].rearrange("n (p t) i j k -> p n (t i j k)", t=4))
+                gts[ch] = g_n
 
-        def coef_load(c):
-            craw = keep.tile([P, 512 * NB], BF16, tag="craw", name="craw%d" % c)
-            nc.sync.dma_start(out=craw[:], in_=coefs[c * P:(c + 1) * P].rearrange("d s b -> d (s b)"))
-            craws[c] = craw
+            def coef_load(c):
+                craw = keep.tile([P, 512 * NB], BF16, tag="craw", name="craw%d" % c)
+                nc.sync.dma_start(out=craw[:], in_=coefs[c * P:(c + 1) * P].rearrange("d s b -> d (s b)"))
+                craws[c] = craw
 
-        def coef_stage(c):
-            cv = craws[c][:].rearrange("d (p y) -> d p y", y=4 * NB)
-            b0 = 0
-            for nbg in (8, 8, 2, 1):
-                cin = work.tile([P, nbg, P, 4], BF16, tag="cin", name="cin%d_%d" % (c, b0), align_bytes=64)
-                for b1 in range(0, nbg, 2):
-                    nb2 = min(2, nbg - b1)
-                    pc = psc.tile([P, nb2, 4, P], BF16, tag="c", name="pc%d_%d" % (c, b0 + b1))
-                    for bi in range(nb2):
-                        for t in range(4):
-                            nc.tensor.transpose(pc[:, bi, t, :], cv[:, :, t * NB + b0 + b1 + bi], ident[:])
-                    nc.scalar.copy(out=cin[:, b1:b1 + nb2], in_=pc[:].rearrange("p b t d -> p b d t"))
-                nc.vector.quantize_mx(
-                    out=ccodes[c][:, b0 * P:(b0 + nbg) * P].bitcast(E4),
-                    scales=cscale[c][:, b0 * P:(b0 + nbg) * P],
-                    in_=cin[:].rearrange("p b d t -> p (b d t)"))
-                b0 += nbg
+            def coef_stage(c):
+                cv = craws[c][:].rearrange("d (p y) -> d p y", y=4 * NB)
+                b0 = 0
+                for nbg in (8, 8, 2, 1):
+                    cin = work.tile([P, nbg, P, 4], BF16, tag="cin", name="cin%d_%d" % (c, b0), align_bytes=64)
+                    for b1 in range(0, nbg, 2):
+                        nb2 = min(2, nbg - b1)
+                        pc = psc.tile([P, nb2, 4, P], BF16, tag="c", name="pc%d_%d" % (c, b0 + b1))
+                        for bi in range(nb2):
+                            for t in range(4):
+                                nc.tensor.transpose(pc[:, bi, t, :], cv[:, :, t * NB + b0 + b1 + bi], ident[:])
+                        nc.scalar.copy(out=cin[:, b1:b1 + nb2], in_=pc[:].rearrange("p b t d -> p b d t"))
+                    nc.vector.quantize_mx(
+                        out=ccodes[c][:, b0 * P:(b0 + nbg) * P].bitcast(E4),
+                        scales=cscale[c][:, b0 * P:(b0 + nbg) * P],
+                        in_=cin[:].rearrange("p b d t -> p (b d t)"))
+                    b0 += nbg
 
-        codes = {}
+            def chunk(ch):
+                n0 = ch * CH
+                nb = n0 // 32
+                g_t = gts[ch]
+                g5 = g_t[:].rearrange("p n (t i c) -> p n t i c", t=4, i=4)
 
-        def chunk(ch):
-            n0 = ch * CH
-            nb = n0 // 32
-            if n0 % 32 == 0:
-                codes[nb] = (
-                    work.tile([P, 4, 512], U32, tag="gcodes", name="gcodes%d" % nb, align_bytes=64),
-                    work.tile([P, 4, 512], U8, tag="gscale", name="gscale%d" % nb, align_bytes=64),
-                    work.tile([P, 3, 512], U32, tag="Gcodes", name="Gcodes%d" % nb, align_bytes=64),
-                    work.tile([P, 3, 512], U8, tag="Gscale", name="Gscale%d" % nb, align_bytes=64))
-            gcodes, gscale, Gcodes, Gscale = codes[nb]
-            g_t = gts[ch]
-            g5 = g_t[:].rearrange("p n (t i c) -> p n t i c", t=4, i=4)
+                flat = g_t[:].rearrange("p n y -> p (n y)")
+                widths = (32, 8, 2)
+                l1s = []
+                gf = []
 
-            flat = g_t[:].rearrange("p n y -> p (n y)")
-            gf = []
-            for q, c1 in enumerate((32, 8, 2)):
-                v1 = flat.rearrange("p (m h c) -> p m h c", h=2, c=c1)
-                l1 = work.tile([P, 2048], F32, tag="l1")
-                nc.vector.tensor_tensor(
-                    out=l1[:].rearrange("p (m c) -> p m c", c=c1), in0=v1[:, :, 0, :], in1=v1[:, :, 1, :], op=ADD)
-                v2 = l1[:].rearrange("p (m h c) -> p m h c", h=2, c=c1 // 2)
-                l2 = l2pool.tile([P, 1024], F32, tag="l2", name="l2_%d_%d" % (ch, q))
-                nc.vector.tensor_tensor(
-                    out=l2[:].rearrange("p (m c) -> p m c", c=c1 // 2), in0=v2[:, :, 0, :], in1=v2[:, :, 1, :], op=ADD)
-                gf.append(l2)
-            gq = work.tile([P, 3, CH, 64], BF16, tag="gq", align_bytes=64)
-            for q in range(3):
-                nc.scalar.copy(
-                    out=gq[:, q].rearrange("p n (c t) -> p n c t", t=4),
-                    in_=gf[q][:].rearrange("p (n t c) -> p n c t", t=4, c=16))
-            wst = work.tile([P, 3, CH, 16], BF16, tag="wst", align_bytes=64)
-            gv0 = gf[0][:].rearrange("p (n t q r) -> p n t q r", t=4, q=4, r=4)
-            gv1 = gf[1][:].rearrange("p (n t q r) -> p n t q r", t=4, q=4, r=4)
-            with nc.allow_low_precision(reason="summed in float32 inside the engine, rounded once to bfloat16"):
-                nc.vector.tensor_reduce(
-                    out=wst[:, 0].rearrange("p n (q t) -> p n q t", t=4),
-                    in_=gv1.rearrange("p n t q r -> p n q t r"), axis=AX.X, op=ADD)
-                nc.vector.tensor_reduce(
-                    out=wst[:, 1].rearrange("p n (q t) -> p n q t", t=4),
-                    in_=gv0.rearrange("p n t q r -> p n q t r"), axis=AX.X, op=ADD)
-                nc.vector.tensor_reduce(
-                    out=wst[:, 2].rearrange("p n (r t) -> p n r t", t=4),
-                    in_=gv0.rearrange("p n t q r -> p n r t q"), axis=AX.X, op=ADD)
+                def level1(q):
+                    v1 = flat.rearrange("p (m h c) -> p m h c", h=2, c=widths[q])
+                    l1 = l1pool.tile([P, 2048], F32, tag="l1", name="l1_%d_%d" % (ch, q))
+                    nc.vector.tensor_tensor(
+                        out=l1[:].rearrange("p (m c) -> p m c", c=widths[q]),
+                        in0=v1[:, :, 0, :], in1=v1[:, :, 1, :], op=ADD)
+                    l1s.append(l1)
 
-            gr = work.tile([P, 4, CH, 16, 4], BF16, tag="gr", align_bytes=64)
-            for i in range(4):
-                nc.scalar.copy(out=gr[:, i], in_=g5[:, :, :, i, :].rearrange("p n t c -> p n c t"))
+                def level2(q):
+                    v2 = l1s[q][:].rearrange("p (m h c) -> p m h c", h=2, c=widths[q] // 2)
+                    l2 = l2pool.tile([P, 1024], F32, tag="l2", name="l2_%d_%d" % (ch, q))
+                    nc.vector.tensor_tensor(
+                        out=l2[:].rearrange("p (m c) -> p m c", c=widths[q] // 2),
+                        in0=v2[:, :, 0, :], in1=v2[:, :, 1, :], op=ADD)
+                    gf.append(l2)
 
-            hsl = slice((n0 % 32) * 16, (n0 % 32 + CH) * 16)
-            for q in range(3):
-                nc.vector.quantize_mx(
-                    out=Gcodes[:, q, hsl].bitcast(E5), scales=Gscale[:, q, hsl],
-                    in_=gq[:, q].rearrange("p n y -> p (n y)"))
-            wsl = slice(n0 * 4, (n0 + CH) * 4)
-            for q in range(3):
-                nc.vector.quantize_mx(
-                    out=Wcodes[q][:, wsl].bitcast(E5), scales=Wscale[q][:, wsl],
-                    in_=wst[:, q].rearrange("p n y -> p (n y)"))
-            for i in range(4):
-                nc.vector.quantize_mx(
-                    out=gcodes[:, i, hsl].bitcast(E5), scales=gscale[:, i, hsl],
-                    in_=gr[:, i].rearrange("p n c t -> p (n c t)"))
+                level1(0)
+                level1(1)
+                level2(0)
+                level1(2)
+                level2(1)
+                level2(2)
+                gq = work.tile([P, 3, CH, 64], BF16, tag="gq", align_bytes=64)
+                for q in range(3):
+                    nc.scalar.copy(
+                        out=gq[:, q].rearrange("p n (c t) -> p n c t", t=4),
+                        in_=gf[q][:].rearrange("p (n t c) -> p n c t", t=4, c=16))
+                wst = work.tile([P, 3, CH, 16], BF16, tag="wst", align_bytes=64)
+                gv0 = gf[0][:].rearrange("p (n t q r) -> p n t q r", t=4, q=4, r=4)
+                gv1 = gf[1][:].rearrange("p (n t q r) -> p n t q r", t=4, q=4, r=4)
+                with nc.allow_low_precision(reason="summed in float32 inside the engine, rounded once to bfloat16"):
+                    nc.vector.tensor_reduce(
+                        out=wst[:, 0].rearrange("p n (q t) -> p n q t", t=4),
+                        in_=gv1.rearrange("p n t q r -> p n q t r"), axis=AX.X, op=ADD)
+                    nc.vector.tensor_reduce(
+                        out=wst[:, 1].rearrange("p n (q t) -> p n q t", t=4),
+                        in_=gv0.rearrange("p n t q r -> p n q t r"), axis=AX.X, op=ADD)
+                    nc.vector.tensor_reduce(
+                        out=wst[:, 2].rearrange("p n (r t) -> p n r t", t=4),
+                        in_=gv0.rearrange("p n t q r -> p n r t q"), axis=AX.X, op=ADD)
 
-        def mx_group(ps, c, terms):
-            last = len(terms) - 1
-            for idx, (b, rc, rs) in enumerate(terms):
-                nc.tensor.matmul_mx(
-                    out=ps,
-                    lhsT=ccodes[c][:, b * P:(b + 1) * P].bitcast(E4),
-                    lhsT_scale=cscale[c][:, b * P:(b + 1) * P],
-                    rhs=rc.bitcast(E5), rhs_scale=rs,
-                    start=(idx == 0), stop=(idx == last))
+                gr = work.tile([P, 4, CH, 16, 4], BF16, tag="gr", align_bytes=64)
+                for i in range(4):
+                    nc.scalar.copy(out=gr[:, i], in_=g5[:, :, :, i, :].rearrange("p n t c -> p n c t"))
 
-        def small_terms(c, nb):
-            gcodes, gscale, Gcodes, Gscale = codes[nb]
+                hsl = slice((n0 % 32) * 16, (n0 % 32 + CH) * 16)
+                gsl = slice(n0 * 16, (n0 + CH) * 16)
+                for q in range(3):
+                    nc.vector.quantize_mx(
+                        out=Gcodes[:, q, gsl].bitcast(E5), scales=Gscale[:, q, gsl],
+                        in_=gq[:, q].rearrange("p n y -> p (n y)"))
+                wsl = slice(n0 * 4, (n0 + CH) * 4)
+                for q in range(3):
+                    nc.vector.quantize_mx(
+                        out=Wcodes[q][:, wsl].bitcast(E5), scales=Wscale[q][:, wsl],
+                        in_=wst[:, q].rearrange("p n y -> p (n y)"))
+                for i in range(4):
+                    nc.vector.quantize_mx(
+                        out=gcodes[:, nb, i, hsl].bitcast(E5), scales=gscale[:, nb, i, hsl],
+                        in_=gr[:, i].rearrange("p n c t -> p (n c t)"))
+
+            def mx_group(ps, c, terms):
+                last = len(terms) - 1
+                for idx, (b, rc, rs) in enumerate(terms):
+                    nc.tensor.matmul_mx(
+                        out=ps,
+                        lhsT=ccodes[c][:, b * P:(b + 1) * P].bitcast(E4),
+                        lhsT_scale=cscale[c][:, b * P:(b + 1) * P],
+                        rhs=rc.bitcast(E5), rhs_scale=rs,
+                        start=(idx == 0), stop=(idx == last))
+
+            g_load(0)
+            coef_load(0)
+            g_load(1)
+            g_load(2)
+            coef_stage(0)
+            coef_load(1)
+            coef_stage(1)
+            for ch in range(NCH):
+                chunk(ch)
+                if ch + GBUFS < NCH:
+                    g_load(ch + GBUFS)
+
+        work2 = ctx.enter_context(tc.tile_pool(name="work2", bufs=2))
+        xpool = ctx.enter_context(tc.tile_pool(name="xpool", bufs=3))
+
+        def gterms(nb):
+            cs = slice(nb * 512, nb * 512 + 512)
+            return [(Gcodes[:, q, cs], Gscale[:, q, cs]) for q in range(3)]
+
+        def u_terms(c):
             usb = []
             for a in range(3):
                 pu = psb.tile([P, 512], F32, tag="b")
                 mx_group(pu[:], c, [(10 + 3 * a + q, Wcodes[q][:], Wscale[q][:]) for q in range(3)])
-                ut = work.tile([P, 32, 4], F32, name="u%d_%d_%d" % (a, c, nb), tag="u%d" % a)
-                nc.scalar.copy(out=ut[:].rearrange("p n q -> p (n q)"), in_=pu[:, nb * P:(nb + 1) * P])
+                ut = work2.tile([P, P, 4], F32, name="u%d_%d" % (a, c), tag="u%d" % a)
+                nc.scalar.copy(out=ut[:].rearrange("p n q -> p (n q)"), in_=pu[:])
                 usb.append(ut)
-            u02 = work.tile([P, 32, 4, 4], F32, tag="u02")
+            u02 = work2.tile([P, P, 4, 4], F32, name="u02_%d" % c, tag="u02")
             nc.gpsimd.tensor_tensor(
-                out=u02[:], in0=usb[0][:].unsqueeze(2).to_broadcast([P, 32, 4, 4]),
-                in1=usb[2][:].unsqueeze(3).to_broadcast([P, 32, 4, 4]), op=ADD)
+                out=u02[:], in0=usb[0][:].unsqueeze(2).to_broadcast([P, P, 4, 4]),
+                in1=usb[2][:].unsqueeze(3).to_broadcast([P, P, 4, 4]), op=ADD)
+            return u02, usb[1]
+
+        def h_terms(c, nb, u02, u1):
+            ns = slice(nb * 32, nb * 32 + 32)
+            gt = gterms(nb)
             p1 = psb.tile([P, 512], F32, tag="b")
-            mx_group(p1[:], c, [(4 + q, Gcodes[:, q, :], Gscale[:, q, :]) for q in range(3)])
-            h1 = work.tile([P, 32, 4, 4], F32, tag="h1")
+            mx_group(p1[:], c, [(4 + q, gt[q][0], gt[q][1]) for q in range(3)])
+            h1 = work2.tile([P, 32, 4, 4], F32, tag="h1")
             nc.vector.tensor_tensor(
-                out=h1[:], in0=p1[:].rearrange("p (n i k) -> p n i k", i=4, k=4), in1=u02[:], op=ADD)
+                out=h1[:], in0=p1[:].rearrange("p (n i k) -> p n i k", i=4, k=4), in1=u02[:, ns], op=ADD)
             p2 = psb.tile([P, 512], F32, tag="b")
-            mx_group(p2[:], c, [(7 + q, Gcodes[:, q, :], Gscale[:, q, :]) for q in range(3)])
-            h2 = work.tile([P, 32, 4, 4], F32, tag="h2")
+            mx_group(p2[:], c, [(7 + q, gt[q][0], gt[q][1]) for q in range(3)])
+            h2 = work2.tile([P, 32, 4, 4], F32, tag="h2")
             nc.vector.tensor_tensor(
                 out=h2[:], in0=p2[:].rearrange("p (n i j) -> p n i j", i=4, j=4),
-                in1=usb[1][:].unsqueeze(2).to_broadcast([P, 32, 4, 4]), op=ADD)
+                in1=u1[:, ns, :].unsqueeze(2).to_broadcast([P, 32, 4, 4]), op=ADD)
             xt = xpool.tile([P, 32, 4, 4, 4], F32, tag="xt", name="xt%d_%d" % (c, nb))
             nc.gpsimd.tensor_tensor(
                 out=xt[:].rearrange("p n i j k -> p (n i) j k"),
@@ -187,12 +219,12 @@ def tile_seteq3to3_t_kernel(tc, x, coefs, bias, grad_out, out):
             return xt
 
         def main_terms(c, nb, xt):
-            gcodes, gscale, Gcodes, Gscale = codes[nb]
             ns = slice(nb * 32, nb * 32 + 32)
+            gt = gterms(nb)
             for i in range(4):
                 pm = psa.tile([P, 512], F32, tag="a")
-                mx_group(pm[:], c, [(0, gcodes[:, i, :], gscale[:, i, :])]
-                         + [(1 + q, Gcodes[:, q, :], Gscale[:, q, :]) for q in range(3)])
+                mx_group(pm[:], c, [(0, gcodes[:, nb, i, :], gscale[:, nb, i, :])]
+                         + [(1 + q, gt[q][0], gt[q][1]) for q in range(3)])
                 xi = xt[:, :, i, :, :].rearrange("p n j k -> p n (j k)")
                 nc.vector.tensor_tensor(
                     out=xi, in0=pm[:].rearrange("p (n y) -> p n y", y=16), in1=xi, op=ADD)
@@ -200,19 +232,14 @@ def tile_seteq3to3_t_kernel(tc, x, coefs, bias, grad_out, out):
                 out=out[ns, c * P:(c + 1) * P].rearrange("n d i j k -> d n (i j k)"),
                 in_=xt[:].rearrange("p n i j k -> p n (i j k)"))
 
-        g_load(0)
-        coef_load(0)
-        g_load(1)
-        g_load(2)
-        coef_stage(0)
-        coef_load(1)
-        coef_stage(1)
-        for ch in range(NCH):
-            chunk(ch)
-            if ch + GBUFS < NCH:
-                g_load(ch + GBUFS)
-            if ch % 2 == 1:
-                nb = ch // 2
-                xts = [small_terms(c, nb) for c in range(2)]
-                for c in range(2):
-                    main_terms(c, nb, xts[c])
+        steps = [(c, nb) for c in range(2) for nb in range(4)]
+        us = {0: u_terms(0)}
+        xts = {0: h_terms(0, 0, us[0][0], us[0][1])}
+        for s in range(8):
+            c, nb = steps[s]
+            if s == 3:
+                us[1] = u_terms(1)
+            if s + 1 < 8:
+                c2, nb2 = steps[s + 1]
+                xts[s + 1] = h_terms(c2, nb2, us[c2][0], us[c2][1])
+            main_terms(c, nb, xts[s])

@@ -33,8 +33,10 @@ def tile_seteq3to3_t_kernel(tc, x, coefs, bias, grad_out, out):
         with ExitStack() as ph1:
             work = ph1.enter_context(tc.tile_pool(name="work", bufs=2))
             gpool = ph1.enter_context(tc.tile_pool(name="gpool", bufs=GBUFS))
-            l1pool = ph1.enter_context(tc.tile_pool(name="l1pool", bufs=3))
-            l2pool = ph1.enter_context(tc.tile_pool(name="l2pool", bufs=4))
+            stage = ph1.enter_context(tc.tile_pool(name="stage", bufs=1))
+            l1pool = ph1.enter_context(tc.tile_pool(name="l1pool", bufs=2))
+            l2pool = ph1.enter_context(tc.tile_pool(name="l2pool", bufs=2))
+            stg = {}
 
             ident = keep.tile([P, P], BF16, name="ident")
             make_identity(nc, ident[:])
@@ -90,7 +92,9 @@ def tile_seteq3to3_t_kernel(tc, x, coefs, bias, grad_out, out):
                 flat = g_t[:].rearrange("p n y -> p (n y)")
                 widths = (32, 8, 2)
                 l1s = []
-                gf = []
+                l2ab = l2pool.tile([P, 2, 1024], F32, tag="l2ab", name="l2ab_%d" % ch)
+                l2c = l2pool.tile([P, 1024], F32, tag="l2c", name="l2c_%d" % ch)
+                gf = [l2ab[:, 0, :], l2ab[:, 1, :], l2c[:]]
 
                 def level1(q):
                     v1 = flat.rearrange("p (m h c) -> p m h c", h=2, c=widths[q])
@@ -102,11 +106,9 @@ def tile_seteq3to3_t_kernel(tc, x, coefs, bias, grad_out, out):
 
                 def level2(q):
                     v2 = l1s[q][:].rearrange("p (m h c) -> p m h c", h=2, c=widths[q] // 2)
-                    l2 = l2pool.tile([P, 1024], F32, tag="l2", name="l2_%d_%d" % (ch, q))
                     nc.vector.tensor_tensor(
-                        out=l2[:].rearrange("p (m c) -> p m c", c=widths[q] // 2),
+                        out=gf[q].rearrange("p (m c) -> p m c", c=widths[q] // 2),
                         in0=v2[:, :, 0, :], in1=v2[:, :, 1, :], op=ADD)
-                    gf.append(l2)
 
                 level1(0)
                 level1(1)
@@ -114,44 +116,46 @@ def tile_seteq3to3_t_kernel(tc, x, coefs, bias, grad_out, out):
                 level1(2)
                 level2(1)
                 level2(2)
-                gq = work.tile([P, 3, CH, 64], BF16, tag="gq", align_bytes=64)
+
+                if n0 % 32 == 0:
+                    stg[nb] = (
+                        stage.tile([P, 3, 32, 64], BF16, tag="gq", name="gq%d" % nb, align_bytes=64),
+                        stage.tile([P, 4, 32, 64], BF16, tag="gr", name="gr%d" % nb, align_bytes=64))
+                gq, gr = stg[nb]
+                wst = work.tile([P, 3, CH, 16], BF16, tag="wst", align_bytes=64)
+                hs = slice(n0 % 32, n0 % 32 + CH)
                 for q in range(3):
                     nc.scalar.copy(
-                        out=gq[:, q].rearrange("p n (c t) -> p n c t", t=4),
-                        in_=gf[q][:].rearrange("p (n t c) -> p n c t", t=4, c=16))
-                wst = work.tile([P, 3, CH, 16], BF16, tag="wst", align_bytes=64)
-                gv0 = gf[0][:].rearrange("p (n t q r) -> p n t q r", t=4, q=4, r=4)
-                gv1 = gf[1][:].rearrange("p (n t q r) -> p n t q r", t=4, q=4, r=4)
+                        out=gq[:, q, hs, :].rearrange("p n (c t) -> p n c t", t=4),
+                        in_=gf[q].rearrange("p (n t c) -> p n c t", t=4, c=16))
                 with nc.allow_low_precision(reason="summed in float32 inside the engine, rounded once to bfloat16"):
                     nc.vector.tensor_reduce(
-                        out=wst[:, 0].rearrange("p n (q t) -> p n q t", t=4),
-                        in_=gv1.rearrange("p n t q r -> p n q t r"), axis=AX.X, op=ADD)
-                    nc.vector.tensor_reduce(
-                        out=wst[:, 1].rearrange("p n (q t) -> p n q t", t=4),
-                        in_=gv0.rearrange("p n t q r -> p n q t r"), axis=AX.X, op=ADD)
+                        out=wst[:, 0:2].rearrange("p g n (q t) -> p (g n) q t", t=4),
+                        in_=l2ab[:].rearrange("p g (n t q r) -> p (g n) q t r", t=4, q=4, r=4), axis=AX.X, op=ADD)
                     nc.vector.tensor_reduce(
                         out=wst[:, 2].rearrange("p n (r t) -> p n r t", t=4),
-                        in_=gv0.rearrange("p n t q r -> p n r t q"), axis=AX.X, op=ADD)
-
-                gr = work.tile([P, 4, CH, 16, 4], BF16, tag="gr", align_bytes=64)
+                        in_=gf[0].rearrange("p (n t q r) -> p n r t q", t=4, q=4, r=4), axis=AX.X, op=ADD)
                 for i in range(4):
-                    nc.scalar.copy(out=gr[:, i], in_=g5[:, :, :, i, :].rearrange("p n t c -> p n c t"))
+                    nc.scalar.copy(
+                        out=gr[:, i, hs, :].rearrange("p n (c t) -> p n c t", t=4),
+                        in_=g5[:, :, :, i, :].rearrange("p n t c -> p n c t"))
 
-                hsl = slice((n0 % 32) * 16, (n0 % 32 + CH) * 16)
-                gsl = slice(n0 * 16, (n0 + CH) * 16)
-                for q in range(3):
-                    nc.vector.quantize_mx(
-                        out=Gcodes[:, q, gsl].bitcast(E5), scales=Gscale[:, q, gsl],
-                        in_=gq[:, q].rearrange("p n y -> p (n y)"))
                 wsl = slice(n0 * 4, (n0 + CH) * 4)
-                for q in range(3):
+                for q, row in ((0, 1), (1, 0), (2, 2)):
                     nc.vector.quantize_mx(
                         out=Wcodes[q][:, wsl].bitcast(E5), scales=Wscale[q][:, wsl],
-                        in_=wst[:, q].rearrange("p n y -> p (n y)"))
-                for i in range(4):
-                    nc.vector.quantize_mx(
-                        out=gcodes[:, nb, i, hsl].bitcast(E5), scales=gscale[:, nb, i, hsl],
-                        in_=gr[:, i].rearrange("p n c t -> p (n c t)"))
+                        in_=wst[:, row].rearrange("p n y -> p (n y)"))
+                if n0 % 32 == CH:
+                    gsl = slice(nb * 512, nb * 512 + 512)
+                    for q in range(3):
+                        nc.vector.quantize_mx(
+                            out=Gcodes[:, q, gsl].bitcast(E5), scales=Gscale[:, q, gsl],
+                            in_=gq[:, q].rearrange("p n y -> p (n y)"))
+                    for a in range(2):
+                        nc.vector.quantize_mx(
+                            out=gcodes[:, nb, 2 * a:2 * a + 2, :].rearrange("p i y -> p (i y)").bitcast(E5),
+                            scales=gscale[:, nb, 2 * a:2 * a + 2, :].rearrange("p i y -> p (i y)"),
+                            in_=gr[:, 2 * a:2 * a + 2].rearrange("p i n y -> p (i n y)"))
 
             def mx_group(ps, c, terms):
                 last = len(terms) - 1

@@ -97,11 +97,15 @@ def tile_seteq3to3_t_kernel(tc, x, coefs, bias, grad_out, out):
                 gf = [l2ab[:, 0, :], l2ab[:, 1, :], l2c[:]]
 
                 def level1(q):
-                    v1 = flat.rearrange("p (m h c) -> p m h c", h=2, c=widths[q])
                     l1 = l1pool.tile([P, 2048], F32, tag="l1", name="l1_%d_%d" % (ch, q))
-                    nc.vector.tensor_tensor(
-                        out=l1[:].rearrange("p (m c) -> p m c", c=widths[q]),
-                        in0=v1[:, :, 0, :], in1=v1[:, :, 1, :], op=ADD)
+                    if q < 2:
+                        v1 = flat.rearrange("p (m h c) -> p m h c", h=2, c=widths[q])
+                        nc.vector.tensor_tensor(
+                            out=l1[:].rearrange("p (m c) -> p m c", c=widths[q]),
+                            in0=v1[:, :, 0, :], in1=v1[:, :, 1, :], op=ADD)
+                    else:
+                        v1 = flat.rearrange("p (m c) -> p m c", c=2)
+                        nc.vector.tensor_tensor(out=l1[:], in0=v1[:, :, 0], in1=v1[:, :, 1], op=ADD)
                     l1s.append(l1)
 
                 def level2(q):
@@ -128,13 +132,21 @@ def tile_seteq3to3_t_kernel(tc, x, coefs, bias, grad_out, out):
                     nc.scalar.copy(
                         out=gq[:, q, hs, :].rearrange("p n (c t) -> p n c t", t=4),
                         in_=gf[q].rearrange("p (n t c) -> p n c t", t=4, c=16))
-                with nc.allow_low_precision(reason="summed in float32 inside the engine, rounded once to bfloat16"):
-                    nc.vector.tensor_reduce(
-                        out=wst[:, 0:2].rearrange("p g n (q t) -> p (g n) q t", t=4),
-                        in_=l2ab[:].rearrange("p g (n t q r) -> p (g n) q t r", t=4, q=4, r=4), axis=AX.X, op=ADD)
-                    nc.vector.tensor_reduce(
-                        out=wst[:, 2].rearrange("p n (r t) -> p n r t", t=4),
-                        in_=gf[0].rearrange("p (n t q r) -> p n r t q", t=4, q=4, r=4), axis=AX.X, op=ADD)
+                wa = l1pool.tile([P, 2048], F32, tag="l1", name="wa_%d" % ch)
+                va = l2ab[:].rearrange("p g (m h c) -> p (g m) h c", h=2, c=2)
+                nc.vector.tensor_tensor(
+                    out=wa[:, 0:1024].rearrange("p (m c) -> p m c", c=2), in0=va[:, :, 0, :], in1=va[:, :, 1, :], op=ADD)
+                vc = gf[0].rearrange("p (m h c) -> p m h c", h=2, c=8)
+                nc.vector.tensor_tensor(
+                    out=wa[:, 1024:1536].rearrange("p (m c) -> p m c", c=8), in0=vc[:, :, 0, :], in1=vc[:, :, 1, :], op=ADD)
+                vb = wa[:, 0:1024].rearrange("p (m t q c) -> p m q t c", t=4, q=4, c=2)
+                nc.vector.tensor_tensor(
+                    out=wst[:, 0:2].rearrange("p g n (q t) -> p (g n) q t", t=4),
+                    in0=vb[:, :, :, :, 0], in1=vb[:, :, :, :, 1], op=ADD)
+                vd = wa[:, 1024:1536].rearrange("p (n t h r) -> p n h r t", t=4, h=2, r=4)
+                nc.vector.tensor_tensor(
+                    out=wst[:, 2].rearrange("p n (r t) -> p n r t", t=4),
+                    in0=vd[:, :, 0, :, :], in1=vd[:, :, 1, :, :], op=ADD)
                 for i in range(4):
                     nc.scalar.copy(
                         out=gr[:, i, hs, :].rearrange("p n (c t) -> p n c t", t=4),

@@ -28,7 +28,8 @@ def tile_seteq3to3_t_kernel(tc, x, coefs, bias, grad_out, out):
     with ExitStack() as ctx:
         keep = ctx.enter_context(tc.tile_pool(name="keep", bufs=1))
         psa = ctx.enter_context(tc.psum_pool(name="psa", bufs=3))
-        psb = ctx.enter_context(tc.psum_pool(name="psb", bufs=3))
+        psb = ctx.enter_context(tc.psum_pool(name="psb", bufs=2))
+        psu = ctx.enter_context(tc.psum_pool(name="psu", bufs=1))
         psc = ctx.enter_context(tc.psum_pool(name="psc", bufs=2))
         with ExitStack() as ph1:
             work = ph1.enter_context(tc.tile_pool(name="work", bufs=2))
@@ -179,6 +180,27 @@ def tile_seteq3to3_t_kernel(tc, x, coefs, bias, grad_out, out):
                         rhs=rc.bitcast(E5), rhs_scale=rs,
                         start=(idx == 0), stop=(idx == last))
 
+            def gterms(nb):
+                cs = slice(nb * 512, nb * 512 + 512)
+                return [(Gcodes[:, q, cs], Gscale[:, q, cs]) for q in range(3)]
+
+            def h_passes(c, nb):
+                gt = gterms(nb)
+                p1 = psb.tile([P, 512], F32, tag="b", name="p1_%d_%d" % (c, nb))
+                mx_group(p1[:], c, [(4 + q, gt[q][0], gt[q][1]) for q in range(3)])
+                p2 = psb.tile([P, 512], F32, tag="b", name="p2_%d_%d" % (c, nb))
+                mx_group(p2[:], c, [(7 + q, gt[q][0], gt[q][1]) for q in range(3)])
+                return p1, p2
+
+            def main_passes(c, nb, i):
+                k = (c * 4 + nb) * 4 + i
+                pool = psa if k % 5 < 3 else psc
+                pm = pool.tile([P, 512], F32, tag="a" if k % 5 < 3 else "c", name="pm%d" % k)
+                gt = gterms(nb)
+                mx_group(pm[:], c, [(0, gcodes[:, nb, i, :], gscale[:, nb, i, :])]
+                         + [(1 + q, gt[q][0], gt[q][1]) for q in range(3)])
+                return pm
+
             g_load(0)
             coef_load(0)
             g_load(1)
@@ -186,46 +208,42 @@ def tile_seteq3to3_t_kernel(tc, x, coefs, bias, grad_out, out):
             coef_stage(0)
             coef_load(1)
             coef_stage(1)
+            early = {}
             for ch in range(NCH):
                 chunk(ch)
                 if ch + GBUFS < NCH:
                     g_load(ch + GBUFS)
+                if ch == 1:
+                    early["h"] = h_passes(0, 0)
+                    early["m"] = [main_passes(0, 0, i) for i in range(4)]
 
         work2 = ctx.enter_context(tc.tile_pool(name="work2", bufs=2))
         xpool = ctx.enter_context(tc.tile_pool(name="xpool", bufs=3))
 
-        def gterms(nb):
-            cs = slice(nb * 512, nb * 512 + 512)
-            return [(Gcodes[:, q, cs], Gscale[:, q, cs]) for q in range(3)]
-
         def u_terms(c):
-            usb = []
-            for a in range(3):
-                pu = psb.tile([P, 512], F32, tag="b")
+            usb = {}
+            for a in (0, 2, 1):
+                pu = psu.tile([P, 512], F32, tag="u", name="pu%d_%d" % (a, c))
                 mx_group(pu[:], c, [(10 + 3 * a + q, Wcodes[q][:], Wscale[q][:]) for q in range(3)])
                 ut = work2.tile([P, P, 4], F32, name="u%d_%d" % (a, c), tag="u%d" % a)
                 nc.scalar.copy(out=ut[:].rearrange("p n q -> p (n q)"), in_=pu[:])
-                usb.append(ut)
-            u02 = work2.tile([P, P, 4, 4], F32, name="u02_%d" % c, tag="u02")
-            nc.gpsimd.tensor_tensor(
-                out=u02[:], in0=usb[0][:].unsqueeze(2).to_broadcast([P, P, 4, 4]),
-                in1=usb[2][:].unsqueeze(3).to_broadcast([P, P, 4, 4]), op=ADD)
-            return u02, usb[1]
+                usb[a] = ut
+            return usb
 
-        def h_terms(c, nb, u02, u1):
+        def h_terms(c, nb, usb, ps):
             ns = slice(nb * 32, nb * 32 + 32)
-            gt = gterms(nb)
-            p1 = psb.tile([P, 512], F32, tag="b")
-            mx_group(p1[:], c, [(4 + q, gt[q][0], gt[q][1]) for q in range(3)])
-            h1 = work2.tile([P, 32, 4, 4], F32, tag="h1")
-            nc.vector.tensor_tensor(
-                out=h1[:], in0=p1[:].rearrange("p (n i k) -> p n i k", i=4, k=4), in1=u02[:, ns], op=ADD)
-            p2 = psb.tile([P, 512], F32, tag="b")
-            mx_group(p2[:], c, [(7 + q, gt[q][0], gt[q][1]) for q in range(3)])
+            p1, p2 = ps
+            u02 = work2.tile([P, 32, 4, 4], F32, tag="u02")
+            nc.gpsimd.tensor_tensor(
+                out=u02[:], in0=usb[0][:, ns, :].unsqueeze(2).to_broadcast([P, 32, 4, 4]),
+                in1=usb[2][:, ns, :].unsqueeze(3).to_broadcast([P, 32, 4, 4]), op=ADD)
             h2 = work2.tile([P, 32, 4, 4], F32, tag="h2")
             nc.vector.tensor_tensor(
                 out=h2[:], in0=p2[:].rearrange("p (n i j) -> p n i j", i=4, j=4),
-                in1=u1[:, ns, :].unsqueeze(2).to_broadcast([P, 32, 4, 4]), op=ADD)
+                in1=usb[1][:, ns, :].unsqueeze(2).to_broadcast([P, 32, 4, 4]), op=ADD)
+            h1 = work2.tile([P, 32, 4, 4], F32, tag="h1")
+            nc.vector.tensor_tensor(
+                out=h1[:], in0=p1[:].rearrange("p (n i k) -> p n i k", i=4, k=4), in1=u02[:], op=ADD)
             xt = xpool.tile([P, 32, 4, 4, 4], F32, tag="xt", name="xt%d_%d" % (c, nb))
             nc.gpsimd.tensor_tensor(
                 out=xt[:].rearrange("p n i j k -> p (n i) j k"),
@@ -234,13 +252,10 @@ def tile_seteq3to3_t_kernel(tc, x, coefs, bias, grad_out, out):
                 op=ADD)
             return xt
 
-        def main_terms(c, nb, xt):
+        def main_terms(c, nb, xt, pms):
             ns = slice(nb * 32, nb * 32 + 32)
-            gt = gterms(nb)
             for i in range(4):
-                pm = psa.tile([P, 512], F32, tag="a")
-                mx_group(pm[:], c, [(0, gcodes[:, nb, i, :], gscale[:, nb, i, :])]
-                         + [(1 + q, gt[q][0], gt[q][1]) for q in range(3)])
+                pm = pms[i] if pms else main_passes(c, nb, i)
                 xi = xt[:, :, i, :, :].rearrange("p n j k -> p n (j k)")
                 nc.vector.tensor_tensor(
                     out=xi, in0=pm[:].rearrange("p (n y) -> p n y", y=16), in1=xi, op=ADD)
@@ -250,12 +265,12 @@ def tile_seteq3to3_t_kernel(tc, x, coefs, bias, grad_out, out):
 
         steps = [(c, nb) for c in range(2) for nb in range(4)]
         us = {0: u_terms(0)}
-        xts = {0: h_terms(0, 0, us[0][0], us[0][1])}
+        xts = {0: h_terms(0, 0, us[0], early["h"])}
         for s in range(8):
             c, nb = steps[s]
             if s == 3:
                 us[1] = u_terms(1)
             if s + 1 < 8:
                 c2, nb2 = steps[s + 1]
-                xts[s + 1] = h_terms(c2, nb2, us[c2][0], us[c2][1])
-            main_terms(c, nb, xts[s])
+                xts[s + 1] = h_terms(c2, nb2, us[c2], h_passes(c2, nb2))
+            main_terms(c, nb, xts[s], early["m"] if s == 0 else None)

@@ -234,7 +234,7 @@ def tile_seteq3to3_t_kernel(tc, x, coefs, bias, grad_out, out):
             ns = slice(nb * 32, nb * 32 + 32)
             p1, p2 = ps
             u02 = work2.tile([P, 32, 4, 4], F32, tag="u02")
-            nc.gpsimd.tensor_tensor(
+            nc.vector.tensor_tensor(
                 out=u02[:], in0=usb[0][:, ns, :].unsqueeze(2).to_broadcast([P, 32, 4, 4]),
                 in1=usb[2][:, ns, :].unsqueeze(3).to_broadcast([P, 32, 4, 4]), op=ADD)
             h2 = work2.tile([P, 32, 4, 4], F32, tag="h2")
@@ -245,7 +245,7 @@ def tile_seteq3to3_t_kernel(tc, x, coefs, bias, grad_out, out):
             nc.vector.tensor_tensor(
                 out=h1[:], in0=p1[:].rearrange("p (n i k) -> p n i k", i=4, k=4), in1=u02[:], op=ADD)
             xt = xpool.tile([P, 32, 4, 4, 4], F32, tag="xt", name="xt%d_%d" % (c, nb))
-            nc.gpsimd.tensor_tensor(
+            nc.vector.tensor_tensor(
                 out=xt[:].rearrange("p n i j k -> p (n i) j k"),
                 in0=h1[:].rearrange("p n i k -> p (n i) k").unsqueeze(2).to_broadcast([P, P, 4, 4]),
                 in1=h2[:].rearrange("p n i j -> p (n i) j").unsqueeze(3).to_broadcast([P, P, 4, 4]),

@@ -21,6 +21,7 @@ NB = 19
 CH = 16
 NCH = 128 // CH
 GBUFS = 3
+PE_CHUNKS = 6
 
 
 def tile_seteq3to3_t_kernel(tc, x, coefs, bias, grad_out, out):
@@ -115,12 +116,15 @@ def tile_seteq3to3_t_kernel(tc, x, coefs, bias, grad_out, out):
                         out=gf[q].rearrange("p (m c) -> p m c", c=widths[q] // 2),
                         in0=v2[:, :, 0, :], in1=v2[:, :, 1, :], op=ADD)
 
+                on_pe = ch < PE_CHUNKS
                 level1(0)
                 level1(1)
                 level2(0)
-                level1(2)
+                if not on_pe:
+                    level1(2)
                 level2(1)
-                level2(2)
+                if not on_pe:
+                    level2(2)
 
                 if n0 % 32 == 0:
                     stg[nb] = (
@@ -129,10 +133,21 @@ def tile_seteq3to3_t_kernel(tc, x, coefs, bias, grad_out, out):
                 gq, gr = stg[nb]
                 wst = work.tile([P, 3, CH, 16], BF16, tag="wst", align_bytes=64)
                 hs = slice(n0 % 32, n0 % 32 + CH)
-                for q in range(3):
+                for q in range(2 if on_pe else 3):
                     nc.scalar.copy(
                         out=gq[:, q, hs, :].rearrange("p n (c t) -> p n c t", t=4),
                         in_=gf[q].rearrange("p (n t c) -> p n c t", t=4, c=16))
+                if on_pe:
+                    for h in range(2):
+                        pk = psu.tile([P, 512], F32, tag="u", name="pk%d_%d" % (ch, h))
+                        vk = g_t[:, h * 8:h * 8 + 8, :].rearrange("p n (m k) -> p n m k", k=4)
+                        for k in range(4):
+                            nc.tensor.matmul(pk[:].rearrange("p (n m) -> p n m", n=8), lhsT=ident[:], rhs=vk[:, :, :, k],
+                                             start=(k == 0), stop=(k == 3))
+                        h0 = n0 % 32 + h * 8
+                        nc.scalar.copy(
+                            out=gq[:, 2, h0:h0 + 8, :].rearrange("p n (c t) -> p n c t", t=4),
+                            in_=pk[:].rearrange("p (n t c) -> p n c t", t=4, c=16))
                 wa = l1pool.tile([P, 2048], F32, tag="l1", name="wa_%d" % ch)
                 va = l2ab[:].rearrange("p g (m h c) -> p (g m) h c", h=2, c=2)
                 nc.vector.tensor_tensor(

@@ -8,13 +8,11 @@ BYTES = 256 * 512 * 19 * 2 + 128 * 512 * 64 * 2 + 128 * 256 * 64 * 4
 
 BF16 = mybir.dt.bfloat16
 F32 = mybir.dt.float32
-I32 = mybir.dt.int32
 U32 = mybir.dt.uint32
 U8 = mybir.dt.uint8
 E4 = mybir.dt.float8_e4m3fn_x4
 E5 = mybir.dt.float8_e5m2_x4
 ADD = mybir.AluOpType.add
-AX = mybir.AxisListType
 
 P = 128
 NB = 19
@@ -22,38 +20,101 @@ CH = 16
 NCH = 128 // CH
 GBUFS = 3
 PE_CHUNKS = 6
+CGROUPS = ((0, 4), (4, 4), (8, 4), (12, 4), (16, 2), (18, 1))
 
 
 def tile_seteq3to3_t_kernel(tc, x, coefs, bias, grad_out, out):
     nc = tc.nc
     with ExitStack() as ctx:
         keep = ctx.enter_context(tc.tile_pool(name="keep", bufs=1))
+        stage = ctx.enter_context(tc.tile_pool(name="stage", bufs=2))
+        upool = ctx.enter_context(tc.tile_pool(name="upool", bufs=2))
         psa = ctx.enter_context(tc.psum_pool(name="psa", bufs=3))
         psb = ctx.enter_context(tc.psum_pool(name="psb", bufs=2))
         psu = ctx.enter_context(tc.psum_pool(name="psu", bufs=1))
         psc = ctx.enter_context(tc.psum_pool(name="psc", bufs=2))
+
+        ident = keep.tile([P, P], BF16, name="ident")
+        make_identity(nc, ident[:])
+
+        Wcodes = [keep.tile([P, 512], U32, name="Wcodes%d" % q, align_bytes=64) for q in range(3)]
+        Wscale = [keep.tile([P, 512], U8, name="Wscale%d" % q, align_bytes=64) for q in range(3)]
+        gcodes = keep.tile([P, 4, 4, 512], U32, name="gcodes", align_bytes=64)
+        gscale = keep.tile([P, 4, 4, 512], U8, name="gscale", align_bytes=64)
+        Gcodes = keep.tile([P, 3, 2048], U32, name="Gcodes", align_bytes=64)
+        Gscale = keep.tile([P, 3, 2048], U8, name="Gscale", align_bytes=64)
+        ccodes = [keep.tile([P, NB * P], U32, name="ccodes%d" % c, align_bytes=64) for c in range(2)]
+        cscale = [keep.tile([P, NB * P], U8, name="cscale%d" % c, align_bytes=64) for c in range(2)]
+
+        gts = {}
+        craws = {}
+        cins = {}
+        stg = {}
+        g01 = {}
+        pks = {}
+
+        def mx_group(ps, c, terms):
+            last = len(terms) - 1
+            for idx, (b, rc, rs) in enumerate(terms):
+                nc.tensor.matmul_mx(
+                    out=ps,
+                    lhsT=ccodes[c][:, b * P:(b + 1) * P].bitcast(E4),
+                    lhsT_scale=cscale[c][:, b * P:(b + 1) * P],
+                    rhs=rc.bitcast(E5), rhs_scale=rs,
+                    start=(idx == 0), stop=(idx == last))
+
+        def gterms(nb):
+            cs = slice(nb * 512, nb * 512 + 512)
+            return [(Gcodes[:, q, cs], Gscale[:, q, cs]) for q in range(3)]
+
+        def h_passes(c, nb):
+            gt = gterms(nb)
+            p1 = psb.tile([P, 512], F32, tag="b", name="p1_%d_%d" % (c, nb))
+            mx_group(p1[:], c, [(4 + q, gt[q][0], gt[q][1]) for q in range(3)])
+            p2 = psb.tile([P, 512], F32, tag="b", name="p2_%d_%d" % (c, nb))
+            mx_group(p2[:], c, [(7 + q, gt[q][0], gt[q][1]) for q in range(3)])
+            return p1, p2
+
+        def main_passes(c, nb, i):
+            k = (c * 4 + nb) * 4 + i
+            pool = psa if k % 5 < 3 else psc
+            pm = pool.tile([P, 512], F32, tag="a" if k % 5 < 3 else "c", name="pm%d" % k)
+            gt = gterms(nb)
+            mx_group(pm[:], c, [(0, gcodes[:, nb, i, :], gscale[:, nb, i, :])]
+                     + [(1 + q, gt[q][0], gt[q][1]) for q in range(3)])
+            return pm
+
+        def u_terms(c):
+            usb = {}
+            for a in (0, 2, 1):
+                pu = psu.tile([P, 512], F32, tag="u", name="pu%d_%d" % (a, c))
+                mx_group(pu[:], c, [(10 + 3 * a + q, Wcodes[q][:], Wscale[q][:]) for q in range(3)])
+                ut = upool.tile([P, P, 4], F32, name="u%d_%d" % (a, c), tag="u%d" % a)
+                nc.scalar.copy(out=ut[:].rearrange("p n q -> p (n q)"), in_=pu[:])
+                usb[a] = ut
+            return usb
+
+        def quant(ch):
+            gq, gr = stg[ch]
+            gsl = slice(ch * 256, ch * 256 + 256)
+            for q in range(3):
+                nc.vector.quantize_mx(
+                    out=Gcodes[:, q, gsl].bitcast(E5), scales=Gscale[:, q, gsl],
+                    in_=gq[:, q].rearrange("p n y -> p (n y)"))
+            nb, half = divmod(ch, 2)
+            hsl = slice(half * 256, half * 256 + 256)
+            for i in range(4):
+                nc.vector.quantize_mx(
+                    out=gcodes[:, nb, i, hsl].bitcast(E5), scales=gscale[:, nb, i, hsl],
+                    in_=gr[:, i].rearrange("p n y -> p (n y)"))
+
         with ExitStack() as ph1:
+            ph1.enter_context(tc.manual_schedule(engines={mybir.EngineType.DVE, mybir.EngineType.Activation}))
             work = ph1.enter_context(tc.tile_pool(name="work", bufs=2))
+            cpool = ph1.enter_context(tc.tile_pool(name="cpool", bufs=4))
             gpool = ph1.enter_context(tc.tile_pool(name="gpool", bufs=GBUFS))
-            stage = ph1.enter_context(tc.tile_pool(name="stage", bufs=1))
             l1pool = ph1.enter_context(tc.tile_pool(name="l1pool", bufs=2))
             l2pool = ph1.enter_context(tc.tile_pool(name="l2pool", bufs=2))
-            stg = {}
-
-            ident = keep.tile([P, P], BF16, name="ident")
-            make_identity(nc, ident[:])
-
-            Wcodes = [keep.tile([P, 512], U32, name="Wcodes%d" % q, align_bytes=64) for q in range(3)]
-            Wscale = [keep.tile([P, 512], U8, name="Wscale%d" % q, align_bytes=64) for q in range(3)]
-            gcodes = keep.tile([P, 4, 4, 512], U32, name="gcodes", align_bytes=64)
-            gscale = keep.tile([P, 4, 4, 512], U8, name="gscale", align_bytes=64)
-            Gcodes = keep.tile([P, 3, 2048], U32, name="Gcodes", align_bytes=64)
-            Gscale = keep.tile([P, 3, 2048], U8, name="Gscale", align_bytes=64)
-            ccodes = [keep.tile([P, NB * P], U32, name="ccodes%d" % c, align_bytes=64) for c in range(2)]
-            cscale = [keep.tile([P, NB * P], U8, name="cscale%d" % c, align_bytes=64) for c in range(2)]
-
-            gts = {}
-            craws = {}
 
             def g_load(ch):
                 g_n = gpool.tile([P, CH, 256], BF16, tag="g", name="g%d" % ch)
@@ -67,36 +128,43 @@ def tile_seteq3to3_t_kernel(tc, x, coefs, bias, grad_out, out):
                 nc.sync.dma_start(out=craw[:], in_=coefs[c * P:(c + 1) * P].rearrange("d s b -> d (s b)"))
                 craws[c] = craw
 
-            def coef_stage(c):
+            def coef_turn(c, g):
+                b0, nbg = CGROUPS[g]
                 cv = craws[c][:].rearrange("d (p y) -> d p y", y=4 * NB)
-                b0 = 0
-                for nbg in (8, 8, 2, 1):
-                    cin = work.tile([P, nbg, P, 4], BF16, tag="cin", name="cin%d_%d" % (c, b0), align_bytes=64)
-                    for b1 in range(0, nbg, 2):
-                        nb2 = min(2, nbg - b1)
-                        pc = psc.tile([P, nb2, 4, P], BF16, tag="c", name="pc%d_%d" % (c, b0 + b1))
-                        for bi in range(nb2):
-                            for t in range(4):
-                                nc.tensor.transpose(pc[:, bi, t, :], cv[:, :, t * NB + b0 + b1 + bi], ident[:])
-                        nc.scalar.copy(out=cin[:, b1:b1 + nb2], in_=pc[:].rearrange("p b t d -> p b d t"))
-                    nc.vector.quantize_mx(
-                        out=ccodes[c][:, b0 * P:(b0 + nbg) * P].bitcast(E4),
-                        scales=cscale[c][:, b0 * P:(b0 + nbg) * P],
-                        in_=cin[:].rearrange("p b d t -> p (b d t)"))
-                    b0 += nbg
+                cin = cpool.tile([P, nbg, P, 4], BF16, tag="cin", name="cin%d_%d" % (c, b0), align_bytes=64)
+                for b1 in range(0, nbg, 2):
+                    nb2 = min(2, nbg - b1)
+                    pc = psc.tile([P, nb2, 4, P], BF16, tag="c", name="pc%d_%d" % (c, b0 + b1))
+                    for bi in range(nb2):
+                        for t in range(4):
+                            nc.tensor.transpose(pc[:, bi, t, :], cv[:, :, t * NB + b0 + b1 + bi], ident[:])
+                    nc.scalar.copy(out=cin[:, b1:b1 + nb2], in_=pc[:].rearrange("p b t d -> p b d t"))
+                cins[(c, g)] = cin
 
-            def chunk(ch):
-                n0 = ch * CH
-                nb = n0 // 32
-                g_t = gts[ch]
-                g5 = g_t[:].rearrange("p n (t i c) -> p n t i c", t=4, i=4)
+            def coef_quant(c, g):
+                b0, nbg = CGROUPS[g]
+                nc.vector.quantize_mx(
+                    out=ccodes[c][:, b0 * P:(b0 + nbg) * P].bitcast(E4),
+                    scales=cscale[c][:, b0 * P:(b0 + nbg) * P],
+                    in_=cins[(c, g)][:].rearrange("p b d t -> p (b d t)"))
 
-                flat = g_t[:].rearrange("p n y -> p (n y)")
+            def pe_g2(ch):
+                pks[ch] = []
+                for h in range(2):
+                    pk = psa.tile([P, 512], F32, tag="a", name="pk%d_%d" % (ch, h))
+                    vk = gts[ch][:, h * 8:h * 8 + 8, :].rearrange("p n (m k) -> p n m k", k=4)
+                    for k in range(4):
+                        nc.tensor.matmul(pk[:].rearrange("p (n m) -> p n m", n=8), lhsT=ident[:], rhs=vk[:, :, :, k],
+                                         start=(k == 0), stop=(k == 3))
+                    pks[ch].append(pk)
+
+            def sums(ch):
+                on_pe = ch < PE_CHUNKS
+                flat = gts[ch][:].rearrange("p n y -> p (n y)")
                 widths = (32, 8, 2)
                 l1s = []
                 l2ab = l2pool.tile([P, 2, 1024], F32, tag="l2ab", name="l2ab_%d" % ch)
-                l2c = l2pool.tile([P, 1024], F32, tag="l2c", name="l2c_%d" % ch)
-                gf = [l2ab[:, 0, :], l2ab[:, 1, :], l2c[:]]
+                g01[ch] = l2ab
 
                 def level1(q):
                     l1 = l1pool.tile([P, 2048], F32, tag="l1", name="l1_%d_%d" % (ch, q))
@@ -113,46 +181,31 @@ def tile_seteq3to3_t_kernel(tc, x, coefs, bias, grad_out, out):
                 def level2(q):
                     v2 = l1s[q][:].rearrange("p (m h c) -> p m h c", h=2, c=widths[q] // 2)
                     nc.vector.tensor_tensor(
-                        out=gf[q].rearrange("p (m c) -> p m c", c=widths[q] // 2),
+                        out=l2ab[:, q, :].rearrange("p (m c) -> p m c", c=widths[q] // 2),
                         in0=v2[:, :, 0, :], in1=v2[:, :, 1, :], op=ADD)
 
-                on_pe = ch < PE_CHUNKS
                 level1(0)
                 level1(1)
                 level2(0)
                 if not on_pe:
                     level1(2)
                 level2(1)
+                if ch >= 2:
+                    quant(ch - 2)
+                gq = stage.tile([P, 3, CH, 64], BF16, tag="gq", name="gq%d" % ch, align_bytes=64)
+                gr = stage.tile([P, 4, CH, 64], BF16, tag="gr", name="gr%d" % ch, align_bytes=64)
+                stg[ch] = (gq, gr)
                 if not on_pe:
-                    level2(2)
-
-                if n0 % 32 == 0:
-                    stg[nb] = (
-                        stage.tile([P, 3, 32, 64], BF16, tag="gq", name="gq%d" % nb, align_bytes=64),
-                        stage.tile([P, 4, 32, 64], BF16, tag="gr", name="gr%d" % nb, align_bytes=64))
-                gq, gr = stg[nb]
-                wst = work.tile([P, 3, CH, 16], BF16, tag="wst", align_bytes=64)
-                hs = slice(n0 % 32, n0 % 32 + CH)
-                for q in range(2 if on_pe else 3):
-                    nc.scalar.copy(
-                        out=gq[:, q, hs, :].rearrange("p n (c t) -> p n c t", t=4),
-                        in_=gf[q].rearrange("p (n t c) -> p n c t", t=4, c=16))
-                if on_pe:
-                    for h in range(2):
-                        pk = psu.tile([P, 512], F32, tag="u", name="pk%d_%d" % (ch, h))
-                        vk = g_t[:, h * 8:h * 8 + 8, :].rearrange("p n (m k) -> p n m k", k=4)
-                        for k in range(4):
-                            nc.tensor.matmul(pk[:].rearrange("p (n m) -> p n m", n=8), lhsT=ident[:], rhs=vk[:, :, :, k],
-                                             start=(k == 0), stop=(k == 3))
-                        h0 = n0 % 32 + h * 8
-                        nc.scalar.copy(
-                            out=gq[:, 2, h0:h0 + 8, :].rearrange("p n (c t) -> p n c t", t=4),
-                            in_=pk[:].rearrange("p (n t c) -> p n c t", t=4, c=16))
+                    v2 = l1s[2][:].rearrange("p (n t c h) -> p n c t h", t=4, c=16, h=2)
+                    nc.vector.tensor_tensor(
+                        out=gq[:, 2].rearrange("p n (c t) -> p n c t", t=4),
+                        in0=v2[:, :, :, :, 0], in1=v2[:, :, :, :, 1], op=ADD)
+                wst = work.tile([P, 3, CH, 16], BF16, tag="wst", name="wst%d" % ch, align_bytes=64)
                 wa = l1pool.tile([P, 2048], F32, tag="l1", name="wa_%d" % ch)
                 va = l2ab[:].rearrange("p g (m h c) -> p (g m) h c", h=2, c=2)
                 nc.vector.tensor_tensor(
                     out=wa[:, 0:1024].rearrange("p (m c) -> p m c", c=2), in0=va[:, :, 0, :], in1=va[:, :, 1, :], op=ADD)
-                vc = gf[0].rearrange("p (m h c) -> p m h c", h=2, c=8)
+                vc = l2ab[:, 0, :].rearrange("p (m h c) -> p m h c", h=2, c=8)
                 nc.vector.tensor_tensor(
                     out=wa[:, 1024:1536].rearrange("p (m c) -> p m c", c=8), in0=vc[:, :, 0, :], in1=vc[:, :, 1, :], op=ADD)
                 vb = wa[:, 0:1024].rearrange("p (m t q c) -> p m q t c", t=4, q=4, c=2)
@@ -163,87 +216,61 @@ def tile_seteq3to3_t_kernel(tc, x, coefs, bias, grad_out, out):
                 nc.vector.tensor_tensor(
                     out=wst[:, 2].rearrange("p n (r t) -> p n r t", t=4),
                     in0=vd[:, :, 0, :, :], in1=vd[:, :, 1, :, :], op=ADD)
-                for i in range(4):
-                    nc.scalar.copy(
-                        out=gr[:, i, hs, :].rearrange("p n (c t) -> p n c t", t=4),
-                        in_=g5[:, :, :, i, :].rearrange("p n t c -> p n c t"))
-
-                wsl = slice(n0 * 4, (n0 + CH) * 4)
+                wsl = slice(ch * 64, ch * 64 + 64)
                 for q, row in ((0, 1), (1, 0), (2, 2)):
                     nc.vector.quantize_mx(
                         out=Wcodes[q][:, wsl].bitcast(E5), scales=Wscale[q][:, wsl],
                         in_=wst[:, row].rearrange("p n y -> p (n y)"))
-                if n0 % 32 == CH:
-                    gsl = slice(nb * 512, nb * 512 + 512)
-                    for q in range(3):
-                        nc.vector.quantize_mx(
-                            out=Gcodes[:, q, gsl].bitcast(E5), scales=Gscale[:, q, gsl],
-                            in_=gq[:, q].rearrange("p n y -> p (n y)"))
-                    for a in range(2):
-                        nc.vector.quantize_mx(
-                            out=gcodes[:, nb, 2 * a:2 * a + 2, :].rearrange("p i y -> p (i y)").bitcast(E5),
-                            scales=gscale[:, nb, 2 * a:2 * a + 2, :].rearrange("p i y -> p (i y)"),
-                            in_=gr[:, 2 * a:2 * a + 2].rearrange("p i n y -> p (i n y)"))
 
-            def mx_group(ps, c, terms):
-                last = len(terms) - 1
-                for idx, (b, rc, rs) in enumerate(terms):
-                    nc.tensor.matmul_mx(
-                        out=ps,
-                        lhsT=ccodes[c][:, b * P:(b + 1) * P].bitcast(E4),
-                        lhsT_scale=cscale[c][:, b * P:(b + 1) * P],
-                        rhs=rc.bitcast(E5), rhs_scale=rs,
-                        start=(idx == 0), stop=(idx == last))
+            def act_copies(ch):
+                gq, gr = stg[ch]
+                for q in range(2):
+                    nc.scalar.copy(
+                        out=gq[:, q].rearrange("p n (c t) -> p n c t", t=4),
+                        in_=g01[ch][:, q, :].rearrange("p (n t c) -> p n c t", t=4, c=16))
+                if ch < PE_CHUNKS:
+                    for h in range(2):
+                        nc.scalar.copy(
+                            out=gq[:, 2, h * 8:h * 8 + 8, :].rearrange("p n (c t) -> p n c t", t=4),
+                            in_=pks[ch][h][:].rearrange("p (n t c) -> p n c t", t=4, c=16))
+                g5 = gts[ch][:].rearrange("p n (t i c) -> p n t i c", t=4, i=4)
+                for i in range(4):
+                    nc.scalar.copy(
+                        out=gr[:, i].rearrange("p n (c t) -> p n c t", t=4),
+                        in_=g5[:, :, :, i, :].rearrange("p n t c -> p n c t"))
 
-            def gterms(nb):
-                cs = slice(nb * 512, nb * 512 + 512)
-                return [(Gcodes[:, q, cs], Gscale[:, q, cs]) for q in range(3)]
-
-            def h_passes(c, nb):
-                gt = gterms(nb)
-                p1 = psb.tile([P, 512], F32, tag="b", name="p1_%d_%d" % (c, nb))
-                mx_group(p1[:], c, [(4 + q, gt[q][0], gt[q][1]) for q in range(3)])
-                p2 = psb.tile([P, 512], F32, tag="b", name="p2_%d_%d" % (c, nb))
-                mx_group(p2[:], c, [(7 + q, gt[q][0], gt[q][1]) for q in range(3)])
-                return p1, p2
-
-            def main_passes(c, nb, i):
-                k = (c * 4 + nb) * 4 + i
-                pool = psa if k % 5 < 3 else psc
-                pm = pool.tile([P, 512], F32, tag="a" if k % 5 < 3 else "c", name="pm%d" % k)
-                gt = gterms(nb)
-                mx_group(pm[:], c, [(0, gcodes[:, nb, i, :], gscale[:, nb, i, :])]
-                         + [(1 + q, gt[q][0], gt[q][1]) for q in range(3)])
-                return pm
-
+            plan = [[(0, 2 * s), (0, 2 * s + 1)] if s < 3 else [(1, s - 3)] for s in range(NCH)]
+            plan[NCH - 1].append((1, 5))
+            early = {}
             g_load(0)
             coef_load(0)
             g_load(1)
-            g_load(2)
-            coef_stage(0)
-            coef_load(1)
-            coef_stage(1)
-            early = {}
-            for ch in range(NCH):
-                chunk(ch)
-                if ch + GBUFS < NCH:
-                    g_load(ch + GBUFS)
-                if ch == 1:
+            for s in range(NCH):
+                if s < PE_CHUNKS:
+                    pe_g2(s)
+                sums(s)
+                if s >= 1:
+                    for c, g in plan[s - 1]:
+                        coef_quant(c, g)
+                    act_copies(s - 1)
+                for c, g in plan[s]:
+                    coef_turn(c, g)
+                if s == 2:
+                    coef_load(1)
+                if s + 2 < NCH:
+                    g_load(s + 2)
+                if s == 4:
                     early["h"] = h_passes(0, 0)
+                if s == NCH - 1:
                     early["m"] = [main_passes(0, 0, i) for i in range(4)]
+            quant(NCH - 2)
+            for c, g in plan[NCH - 1]:
+                coef_quant(c, g)
+            us = {0: u_terms(0)}
+            act_copies(NCH - 1)
 
         work2 = ctx.enter_context(tc.tile_pool(name="work2", bufs=2))
         xpool = ctx.enter_context(tc.tile_pool(name="xpool", bufs=3))
-
-        def u_terms(c):
-            usb = {}
-            for a in (0, 2, 1):
-                pu = psu.tile([P, 512], F32, tag="u", name="pu%d_%d" % (a, c))
-                mx_group(pu[:], c, [(10 + 3 * a + q, Wcodes[q][:], Wscale[q][:]) for q in range(3)])
-                ut = work2.tile([P, P, 4], F32, name="u%d_%d" % (a, c), tag="u%d" % a)
-                nc.scalar.copy(out=ut[:].rearrange("p n q -> p (n q)"), in_=pu[:])
-                usb[a] = ut
-            return usb
 
         def h_terms(c, nb, usb, ps):
             ns = slice(nb * 32, nb * 32 + 32)
@@ -279,10 +306,11 @@ def tile_seteq3to3_t_kernel(tc, x, coefs, bias, grad_out, out):
                 in_=xt[:].rearrange("p n i j k -> p n (i j k)"))
 
         steps = [(c, nb) for c in range(2) for nb in range(4)]
-        us = {0: u_terms(0)}
         xts = {0: h_terms(0, 0, us[0], early["h"])}
         for s in range(8):
             c, nb = steps[s]
+            if s == 1:
+                quant(NCH - 1)
             if s == 3:
                 us[1] = u_terms(1)
             if s + 1 < 8:

@@ -19,6 +19,7 @@ NB = 19
 CH = 16
 NCH = 128 // CH
 GBUFS = 3
+GP_N = 16
 PE_CHUNKS = 6
 CGROUPS = ((0, 4), (4, 4), (8, 4), (12, 4), (16, 2), (18, 1))
 
@@ -276,7 +277,7 @@ def tile_seteq3to3_t_kernel(tc, x, coefs, bias, grad_out, out):
             ns = slice(nb * 32, nb * 32 + 32)
             p1, p2 = ps
             u02 = work2.tile([P, 32, 4, 4], F32, tag="u02")
-            nc.vector.tensor_tensor(
+            nc.gpsimd.tensor_tensor(
                 out=u02[:], in0=usb[0][:, ns, :].unsqueeze(2).to_broadcast([P, 32, 4, 4]),
                 in1=usb[2][:, ns, :].unsqueeze(3).to_broadcast([P, 32, 4, 4]), op=ADD)
             h2 = work2.tile([P, 32, 4, 4], F32, tag="h2")
@@ -287,11 +288,13 @@ def tile_seteq3to3_t_kernel(tc, x, coefs, bias, grad_out, out):
             nc.vector.tensor_tensor(
                 out=h1[:], in0=p1[:].rearrange("p (n i k) -> p n i k", i=4, k=4), in1=u02[:], op=ADD)
             xt = xpool.tile([P, 32, 4, 4, 4], F32, tag="xt", name="xt%d_%d" % (c, nb))
-            nc.vector.tensor_tensor(
-                out=xt[:].rearrange("p n i j k -> p (n i) j k"),
-                in0=h1[:].rearrange("p n i k -> p (n i) k").unsqueeze(2).to_broadcast([P, P, 4, 4]),
-                in1=h2[:].rearrange("p n i j -> p (n i) j").unsqueeze(3).to_broadcast([P, P, 4, 4]),
-                op=ADD)
+            for eng, n1, n2 in ((nc.gpsimd, 0, GP_N), (nc.vector, GP_N, 32)):
+                rows = (n2 - n1) * 4
+                eng.tensor_tensor(
+                    out=xt[:, n1:n2].rearrange("p n i j k -> p (n i) j k"),
+                    in0=h1[:, n1:n2].rearrange("p n i k -> p (n i) k").unsqueeze(2).to_broadcast([P, rows, 4, 4]),
+                    in1=h2[:, n1:n2].rearrange("p n i j -> p (n i) j").unsqueeze(3).to_broadcast([P, rows, 4, 4]),
+                    op=ADD)
             return xt
 
         def main_terms(c, nb, xt, pms):

from contextlib import ExitStack

import concourse.mybir as mybir
from concourse.masks import make_identity

FLOPS = 2 * 256 * 512 * (8192 + 9 * 2048 + 9 * 512)
BYTES = 256 * 512 * 19 * 2 + 128 * 512 * 64 * 2 + 128 * 256 * 64 * 4

BF16 = mybir.dt.bfloat16
F32 = mybir.dt.float32
U32 = mybir.dt.uint32
U8 = mybir.dt.uint8
E4 = mybir.dt.float8_e4m3fn_x4
E5 = mybir.dt.float8_e5m2_x4
ADD = mybir.AluOpType.add

P = 128
NB = 19
CH = 16
NCH = 128 // CH
GBUFS = 3
GP_N = 16
PE_CHUNKS = 6
CGROUPS = ((0, 4), (4, 4), (8, 4), (12, 4), (16, 2), (18, 1))


def tile_seteq3to3_t_kernel(tc, x, coefs, bias, grad_out, out):
    nc = tc.nc
    with ExitStack() as ctx:
        keep = ctx.enter_context(tc.tile_pool(name="keep", bufs=1))
        stage = ctx.enter_context(tc.tile_pool(name="stage", bufs=2))
        upool = ctx.enter_context(tc.tile_pool(name="upool", bufs=2))
        psa = ctx.enter_context(tc.psum_pool(name="psa", bufs=3))
        psb = ctx.enter_context(tc.psum_pool(name="psb", bufs=2))
        psu = ctx.enter_context(tc.psum_pool(name="psu", bufs=1))
        psc = ctx.enter_context(tc.psum_pool(name="psc", bufs=2))

        ident = keep.tile([P, P], BF16, name="ident")
        make_identity(nc, ident[:])

        Wcodes = [keep.tile([P, 512], U32, name="Wcodes%d" % q, align_bytes=64) for q in range(3)]
        Wscale = [keep.tile([P, 512], U8, name="Wscale%d" % q, align_bytes=64) for q in range(3)]
        gcodes = keep.tile([P, 4, 4, 512], U32, name="gcodes", align_bytes=64)
        gscale = keep.tile([P, 4, 4, 512], U8, name="gscale", align_bytes=64)
        Gcodes = keep.tile([P, 3, 2048], U32, name="Gcodes", align_bytes=64)
        Gscale = keep.tile([P, 3, 2048], U8, name="Gscale", align_bytes=64)
        ccodes = [keep.tile([P, NB * P], U32, name="ccodes%d" % c, align_bytes=64) for c in range(2)]
        cscale = [keep.tile([P, NB * P], U8, name="cscale%d" % c, align_bytes=64) for c in range(2)]

        gts = {}
        craws = {}
        cins = {}
        stg = {}
        g01 = {}
        pks = {}

        def mx_group(ps, c, terms):
            last = len(terms) - 1
            for idx, (b, rc, rs) in enumerate(terms):
                nc.tensor.matmul_mx(
                    out=ps,
                    lhsT=ccodes[c][:, b * P:(b + 1) * P].bitcast(E4),
                    lhsT_scale=cscale[c][:, b * P:(b + 1) * P],
                    rhs=rc.bitcast(E5), rhs_scale=rs,
                    start=(idx == 0), stop=(idx == last))

        def gterms(nb):
            cs = slice(nb * 512, nb * 512 + 512)
            return [(Gcodes[:, q, cs], Gscale[:, q, cs]) for q in range(3)]

        def h_passes(c, nb):
            gt = gterms(nb)
            p1 = psb.tile([P, 512], F32, tag="b", name="p1_%d_%d" % (c, nb))
            mx_group(p1[:], c, [(4 + q, gt[q][0], gt[q][1]) for q in range(3)])
            p2 = psb.tile([P, 512], F32, tag="b", name="p2_%d_%d" % (c, nb))
            mx_group(p2[:], c, [(7 + q, gt[q][0], gt[q][1]) for q in range(3)])
            return p1, p2

        def main_passes(c, nb, i):
            k = (c * 4 + nb) * 4 + i
            pool = psa if k % 5 < 3 else psc
            pm = pool.tile([P, 512], F32, tag="a" if k % 5 < 3 else "c", name="pm%d" % k)
            gt = gterms(nb)
            mx_group(pm[:], c, [(0, gcodes[:, nb, i, :], gscale[:, nb, i, :])]
                     + [(1 + q, gt[q][0], gt[q][1]) for q in range(3)])
            return pm

        def u_terms(c):
            usb = {}
            for a in (0, 2, 1):
                pu = psu.tile([P, 512], F32, tag="u", name="pu%d_%d" % (a, c))
                mx_group(pu[:], c, [(10 + 3 * a + q, Wcodes[q][:], Wscale[q][:]) for q in range(3)])
                ut = upool.tile([P, P, 4], F32, name="u%d_%d" % (a, c), tag="u%d" % a)
                nc.scalar.copy(out=ut[:].rearrange("p n q -> p (n q)"), in_=pu[:])
                usb[a] = ut
            return usb

        def quant(ch):
            gq, gr = stg[ch]
            gsl = slice(ch * 256, ch * 256 + 256)
            for q in range(3):
                nc.vector.quantize_mx(
                    out=Gcodes[:, q, gsl].bitcast(E5), scales=Gscale[:, q, gsl],
                    in_=gq[:, q].rearrange("p n y -> p (n y)"))
            nb, half = divmod(ch, 2)
            hsl = slice(half * 256, half * 256 + 256)
            for i in range(4):
                nc.vector.quantize_mx(
                    out=gcodes[:, nb, i, hsl].bitcast(E5), scales=gscale[:, nb, i, hsl],
                    in_=gr[:, i].rearrange("p n y -> p (n y)"))

        with ExitStack() as ph1:
            ph1.enter_context(tc.manual_schedule(engines={mybir.EngineType.DVE, mybir.EngineType.Activation}))
            work = ph1.enter_context(tc.tile_pool(name="work", bufs=2))
            cpool = ph1.enter_context(tc.tile_pool(name="cpool", bufs=4))
            gpool = ph1.enter_context(tc.tile_pool(name="gpool", bufs=GBUFS))
            l1pool = ph1.enter_context(tc.tile_pool(name="l1pool", bufs=2))
            l2pool = ph1.enter_context(tc.tile_pool(name="l2pool", bufs=2))

            def g_load(ch):
                g_n = gpool.tile([P, CH, 256], BF16, tag="g", name="g%d" % ch)
                nc.sync.dma_start(
                    out=g_n[:],
                    in_=grad_out[ch * CH:(ch + 1) * CH].rearrange("n (p t) i j k -> p n (t i j k)", t=4))
                gts[ch] = g_n

            def coef_load(c):
                craw = keep.tile([P, 512 * NB], BF16, tag="craw", name="craw%d" % c)
                nc.sync.dma_start(out=craw[:], in_=coefs[c * P:(c + 1) * P].rearrange("d s b -> d (s b)"))
                craws[c] = craw

            def coef_turn(c, g):
                b0, nbg = CGROUPS[g]
                cv = craws[c][:].rearrange("d (p y) -> d p y", y=4 * NB)
                cin = cpool.tile([P, nbg, P, 4], BF16, tag="cin", name="cin%d_%d" % (c, b0), align_bytes=64)
                for b1 in range(0, nbg, 2):
                    nb2 = min(2, nbg - b1)
                    pc = psc.tile([P, nb2, 4, P], BF16, tag="c", name="pc%d_%d" % (c, b0 + b1))
                    for bi in range(nb2):
                        for t in range(4):
                            nc.tensor.transpose(pc[:, bi, t, :], cv[:, :, t * NB + b0 + b1 + bi], ident[:])
                    nc.scalar.copy(out=cin[:, b1:b1 + nb2], in_=pc[:].rearrange("p b t d -> p b d t"))
                cins[(c, g)] = cin

            def coef_quant(c, g):
                b0, nbg = CGROUPS[g]
                nc.vector.quantize_mx(
                    out=ccodes[c][:, b0 * P:(b0 + nbg) * P].bitcast(E4),
                    scales=cscale[c][:, b0 * P:(b0 + nbg) * P],
                    in_=cins[(c, g)][:].rearrange("p b d t -> p (b d t)"))

            def pe_g2(ch):
                pks[ch] = []
                for h in range(2):
                    pk = psa.tile([P, 512], F32, tag="a", name="pk%d_%d" % (ch, h))
                    vk = gts[ch][:, h * 8:h * 8 + 8, :].rearrange("p n (m k) -> p n m k", k=4)
                    for k in range(4):
                        nc.tensor.matmul(pk[:].rearrange("p (n m) -> p n m", n=8), lhsT=ident[:], rhs=vk[:, :, :, k],
                                         start=(k == 0), stop=(k == 3))
                    pks[ch].append(pk)

            def sums(ch):
                on_pe = ch < PE_CHUNKS
                flat = gts[ch][:].rearrange("p n y -> p (n y)")
                widths = (32, 8, 2)
                l1s = []
                l2ab = l2pool.tile([P, 2, 1024], F32, tag="l2ab", name="l2ab_%d" % ch)
                g01[ch] = l2ab

                def level1(q):
                    l1 = l1pool.tile([P, 2048], F32, tag="l1", name="l1_%d_%d" % (ch, q))
                    if q < 2:
                        v1 = flat.rearrange("p (m h c) -> p m h c", h=2, c=widths[q])
                        nc.vector.tensor_tensor(
                            out=l1[:].rearrange("p (m c) -> p m c", c=widths[q]),
                            in0=v1[:, :, 0, :], in1=v1[:, :, 1, :], op=ADD)
                    else:
                        v1 = flat.rearrange("p (m c) -> p m c", c=2)
                        nc.vector.tensor_tensor(out=l1[:], in0=v1[:, :, 0], in1=v1[:, :, 1], op=ADD)
                    l1s.append(l1)

                def level2(q):
                    v2 = l1s[q][:].rearrange("p (m h c) -> p m h c", h=2, c=widths[q] // 2)
                    nc.vector.tensor_tensor(
                        out=l2ab[:, q, :].rearrange("p (m c) -> p m c", c=widths[q] // 2),
                        in0=v2[:, :, 0, :], in1=v2[:, :, 1, :], op=ADD)

                level1(0)
                level1(1)
                level2(0)
                if not on_pe:
                    level1(2)
                level2(1)
                if ch >= 2:
                    quant(ch - 2)
                gq = stage.tile([P, 3, CH, 64], BF16, tag="gq", name="gq%d" % ch, align_bytes=64)
                gr = stage.tile([P, 4, CH, 64], BF16, tag="gr", name="gr%d" % ch, align_bytes=64)
                stg[ch] = (gq, gr)
                if not on_pe:
                    v2 = l1s[2][:].rearrange("p (n t c h) -> p n c t h", t=4, c=16, h=2)
                    nc.vector.tensor_tensor(
                        out=gq[:, 2].rearrange("p n (c t) -> p n c t", t=4),
                        in0=v2[:, :, :, :, 0], in1=v2[:, :, :, :, 1], op=ADD)
                wst = work.tile([P, 3, CH, 16], BF16, tag="wst", name="wst%d" % ch, align_bytes=64)
                wa = l1pool.tile([P, 2048], F32, tag="l1", name="wa_%d" % ch)
                va = l2ab[:].rearrange("p g (m h c) -> p (g m) h c", h=2, c=2)
                nc.vector.tensor_tensor(
                    out=wa[:, 0:1024].rearrange("p (m c) -> p m c", c=2), in0=va[:, :, 0, :], in1=va[:, :, 1, :], op=ADD)
                vc = l2ab[:, 0, :].rearrange("p (m h c) -> p m h c", h=2, c=8)
                nc.vector.tensor_tensor(
                    out=wa[:, 1024:1536].rearrange("p (m c) -> p m c", c=8), in0=vc[:, :, 0, :], in1=vc[:, :, 1, :], op=ADD)
                vb = wa[:, 0:1024].rearrange("p (m t q c) -> p m q t c", t=4, q=4, c=2)
                nc.vector.tensor_tensor(
                    out=wst[:, 0:2].rearrange("p g n (q t) -> p (g n) q t", t=4),
                    in0=vb[:, :, :, :, 0], in1=vb[:, :, :, :, 1], op=ADD)
                vd = wa[:, 1024:1536].rearrange("p (n t h r) -> p n h r t", t=4, h=2, r=4)
                nc.vector.tensor_tensor(
                    out=wst[:, 2].rearrange("p n (r t) -> p n r t", t=4),
                    in0=vd[:, :, 0, :, :], in1=vd[:, :, 1, :, :], op=ADD)
                wsl = slice(ch * 64, ch * 64 + 64)
                for q, row in ((0, 1), (1, 0), (2, 2)):
                    nc.vector.quantize_mx(
                        out=Wcodes[q][:, wsl].bitcast(E5), scales=Wscale[q][:, wsl],
                        in_=wst[:, row].rearrange("p n y -> p (n y)"))

            def act_copies(ch):
                gq, gr = stg[ch]
                for q in range(2):
                    nc.scalar.copy(
                        out=gq[:, q].rearrange("p n (c t) -> p n c t", t=4),
                        in_=g01[ch][:, q, :].rearrange("p (n t c) -> p n c t", t=4, c=16))
                if ch < PE_CHUNKS:
                    for h in range(2):
                        nc.scalar.copy(
                            out=gq[:, 2, h * 8:h * 8 + 8, :].rearrange("p n (c t) -> p n c t", t=4),
                            in_=pks[ch][h][:].rearrange("p (n t c) -> p n c t", t=4, c=16))
                g5 = gts[ch][:].rearrange("p n (t i c) -> p n t i c", t=4, i=4)
                for i in range(4):
                    nc.scalar.copy(
                        out=gr[:, i].rearrange("p n (c t) -> p n c t", t=4),
                        in_=g5[:, :, :, i, :].rearrange("p n t c -> p n c t"))

            plan = [[(0, 2 * s), (0, 2 * s + 1)] if s < 3 else [(1, s - 3)] for s in range(NCH)]
            plan[NCH - 1].append((1, 5))
            early = {}
            g_load(0)
            coef_load(0)
            g_load(1)
            for s in range(NCH):
                if s < PE_CHUNKS:
                    pe_g2(s)
                sums(s)
                if s >= 1:
                    for c, g in plan[s - 1]:
                        coef_quant(c, g)
                    act_copies(s - 1)
                for c, g in plan[s]:
                    coef_turn(c, g)
                if s == 2:
                    coef_load(1)
                if s + 2 < NCH:
                    g_load(s + 2)
                if s == 4:
                    early["h"] = h_passes(0, 0)
                if s == NCH - 1:
                    early["m"] = [main_passes(0, 0, i) for i in range(4)]
            quant(NCH - 2)
            for c, g in plan[NCH - 1]:
                coef_quant(c, g)
            us = {0: u_terms(0)}
            act_copies(NCH - 1)

        work2 = ctx.enter_context(tc.tile_pool(name="work2", bufs=2))
        xpool = ctx.enter_context(tc.tile_pool(name="xpool", bufs=3))

        def h_terms(c, nb, usb, ps):
            ns = slice(nb * 32, nb * 32 + 32)
            p1, p2 = ps
            u02 = work2.tile([P, 32, 4, 4], F32, tag="u02")
            nc.gpsimd.tensor_tensor(
                out=u02[:], in0=usb[0][:, ns, :].unsqueeze(2).to_broadcast([P, 32, 4, 4]),
                in1=usb[2][:, ns, :].unsqueeze(3).to_broadcast([P, 32, 4, 4]), op=ADD)
            h2 = work2.tile([P, 32, 4, 4], F32, tag="h2")
            nc.vector.tensor_tensor(
                out=h2[:], in0=p2[:].rearrange("p (n i j) -> p n i j", i=4, j=4),
                in1=usb[1][:, ns, :].unsqueeze(2).to_broadcast([P, 32, 4, 4]), op=ADD)
            h1 = work2.tile([P, 32, 4, 4], F32, tag="h1")
            nc.vector.tensor_tensor(
                out=h1[:], in0=p1[:].rearrange("p (n i k) -> p n i k", i=4, k=4), in1=u02[:], op=ADD)
            xt = xpool.tile([P, 32, 4, 4, 4], F32, tag="xt", name="xt%d_%d" % (c, nb))
            for eng, n1, n2 in ((nc.gpsimd, 0, GP_N), (nc.vector, GP_N, 32)):
                rows = (n2 - n1) * 4
                eng.tensor_tensor(
                    out=xt[:, n1:n2].rearrange("p n i j k -> p (n i) j k"),
                    in0=h1[:, n1:n2].rearrange("p n i k -> p (n i) k").unsqueeze(2).to_broadcast([P, rows, 4, 4]),
                    in1=h2[:, n1:n2].rearrange("p n i j -> p (n i) j").unsqueeze(3).to_broadcast([P, rows, 4, 4]),
                    op=ADD)
            return xt

        def main_terms(c, nb, xt, pms):
            ns = slice(nb * 32, nb * 32 + 32)
            for i in range(4):
                pm = pms[i] if pms else main_passes(c, nb, i)
                xi = xt[:, :, i, :, :].rearrange("p n j k -> p n (j k)")
                nc.vector.tensor_tensor(
                    out=xi, in0=pm[:].rearrange("p (n y) -> p n y", y=16), in1=xi, op=ADD)
            nc.sync.dma_start(
                out=out[ns, c * P:(c + 1) * P].rearrange("n d i j k -> d n (i j k)"),
                in_=xt[:].rearrange("p n i j k -> p n (i j k)"))

        steps = [(c, nb) for c in range(2) for nb in range(4)]
        xts = {0: h_terms(0, 0, us[0], early["h"])}
        for s in range(8):
            c, nb = steps[s]
            if s == 1:
                quant(NCH - 1)
            if s == 3:
                us[1] = u_terms(1)
            if s + 1 < 8:
                c2, nb2 = steps[s + 1]
                xts[s + 1] = h_terms(c2, nb2, us[c2], h_passes(c2, nb2))
            main_terms(c, nb, xts[s], early["m"] if s == 0 else None)
